import numpy as np
import ml_dtypes


def mxq(x, axis, fmt="e4m3"):
    dtype, down = {"e4m3": (ml_dtypes.float8_e4m3fn, 7), "e5m2": (ml_dtypes.float8_e5m2, 14)}[fmt]
    v = np.moveaxis(np.asarray(x, np.float32).astype(ml_dtypes.bfloat16).astype(np.float64), axis, -1)
    blocks = v.reshape(v.shape[:-1] + (-1, 32))
    amax = np.abs(blocks).max(-1, keepdims=True)
    byte = np.maximum(np.where(amax > 0, np.frexp(amax)[1] - 1 + 127, 0) - down, 1)
    scale = np.exp2(byte - 127.0)
    codes = (blocks / scale).astype(np.float32).astype(dtype).astype(np.float64)
    return np.moveaxis((codes * scale).reshape(v.shape), -1, axis)


WIDE = False


def mx_kscale(k):
    if not WIDE:
        return np.ones(k)
    levels = np.array([10, -10, 5, -5, 0])
    if k % 512:
        return np.exp2(np.random.permutation(np.resize(levels, k // 32))).repeat(32)
    a = np.empty((k // 512, 16))
    for p in range(k // 512):
        a[p, :8] = np.random.permutation(np.resize(levels, 8))
        for g in range(8):
            far = levels[np.abs(levels - a[p, g]) >= 10]
            a[p, g + 8] = far[np.random.randint(len(far))]
    return np.exp2(a.ravel()).repeat(32)


BF16 = ml_dtypes.bfloat16


def bf(x):
    return np.asarray(x, np.float32).astype(BF16)


def f64(x):
    return np.asarray(x).astype(np.float64)


H, L, B, S = 512, 2, 1024, 16


def sigmoid(v):
    return 1.0 / (1.0 + np.exp(-v))


def setup_inputs():
    r = np.random.standard_normal
    s, t, u = mx_kscale(H), mx_kscale(H), mx_kscale(H)
    st = np.concatenate([s, t])
    return {
        "x": bf(r((B, H)) * s),
        "enc_seq": bf(r((S, B, H)) * t),
        "attn_W": bf(r((H, H)) / np.sqrt(H) / s[None, :] / t[:, None]),
        "attn_b": bf(r(H) * 0.5 / t),
        "h_prev": bf(r((B, H)) * u),
        "c_prev": bf(r((B, H))),
        "W_ih0": bf(r((4 * H, H + H)) * 0.6 / np.sqrt(H) / st[None, :]),
        "W_hh0": bf(r((4 * H, H)) * 0.6 / np.sqrt(H) / u[None, :]),
        "b_ih0": bf(r(4 * H) * 0.3),
        "b_hh0": bf(r(4 * H) * 0.3),
    }


def reference(x, enc_seq, attn_W, attn_b, h_prev, c_prev, W_ih0, W_hh0, b_ih0, b_hh0):
    enc = f64(enc_seq)
    xq = mxq(f64(x), 1, "e4m3")
    attn_lin = (xq @ mxq(f64(attn_W).T, 0, "e4m3")) + f64(attn_b)
    scores = attn_lin[None, :, :] * enc
    e = np.exp(scores - scores.max(0, keepdims=True))
    w = e / e.sum(0, keepdims=True)
    attention = (enc * w).sum(0)
    aq = mxq(attention, 1, "e4m3")
    w_x = mxq(f64(W_ih0)[:, :H].T, 0, "e4m3")
    w_a = mxq(f64(W_ih0)[:, H:].T, 0, "e4m3")
    hq = mxq(f64(h_prev), 1, "e4m3")
    gates = (xq @ w_x) + (aq @ w_a) + f64(b_ih0) + (hq @ mxq(f64(W_hh0).T, 0, "e4m3")) + f64(b_hh0)
    i, f, g, o = np.split(gates, 4, axis=-1)
    c_new = sigmoid(f) * f64(c_prev) + sigmoid(i) * np.tanh(g)
    h_new = sigmoid(o) * np.tanh(c_new)
    return h_new, c_new

@@ -1,0 +1,387 @@
+from contextlib import ExitStack
+
+import concourse.mybir as mybir
+from concourse.masks import make_identity
+
+BF16 = mybir.dt.bfloat16
+F32 = mybir.dt.float32
+U32 = mybir.dt.uint32
+U8 = mybir.dt.uint8
+I32 = mybir.dt.int32
+FP8X4 = mybir.dt.float8_e4m3fn_x4
+ALU = mybir.AluOpType
+FUNC = mybir.ActivationFunctionType
+INNER_TWO = mybir.AxisListType.XY
+
+P = 128
+PACK = 4
+K_PASS = P * PACK
+B, H, S = 1024, 512, 16
+N_BT = B // P
+N_JC = H // P
+N_CHUNKS = N_BT * N_JC
+N_GATES = 4
+GATE_I, GATE_F, GATE_G, GATE_O = 0, 1, 2, 3
+N_GC = N_GATES * N_JC
+S_RUN = 4
+S_OUT = S // S_RUN
+GATE_SCALE = (0.5, 0.5, 1.0, 0.5)
+
+FLOPS = 2 * B * H * H + 2 * B * (3 * H) * (N_GATES * H)
+
+
+def tile_decoderlstm_pa_t_kernel(
+    tc, x, enc_seq, attn_W, attn_b, h_prev, c_prev, W_ih0, W_hh0, b_ih0, b_hh0, out_0, out_1
+):
+    nc = tc.nc
+    with ExitStack() as ctx:
+        keep = ctx.enter_context(tc.tile_pool(name="keep", bufs=1))
+        raw_pool = ctx.enter_context(tc.tile_pool(name="raw", bufs=2))
+        grouped_pool = ctx.enter_context(tc.tile_pool(name="grouped", bufs=3))
+        enc_pool = ctx.enter_context(tc.tile_pool(name="enc", bufs=2))
+        soft_pool = ctx.enter_context(tc.tile_pool(name="soft", bufs=4))
+        prod_pool = ctx.enter_context(tc.tile_pool(name="prod", bufs=2))
+        row_pool = ctx.enter_context(tc.tile_pool(name="row", bufs=2))
+        cell_pool = ctx.enter_context(tc.tile_pool(name="cell", bufs=1))
+        out_pool = ctx.enter_context(tc.tile_pool(name="out", bufs=2))
+        psum_lin = ctx.enter_context(tc.psum_pool(name="psum_lin", bufs=2))
+        psum_gates = ctx.enter_context(tc.psum_pool(name="psum_gates", bufs=2))
+        psum_move = ctx.enter_context(tc.psum_pool(name="psum_move", bufs=4))
+
+        ident_bf = keep.tile([P, P], BF16)
+        make_identity(nc, ident_bf[:])
+        ident_f32 = keep.tile([P, P], F32)
+        make_identity(nc, ident_f32[:])
+
+        bias_rows = keep.tile([P, P], BF16)
+        nc.vector.memset(bias_rows[:].bitcast(I32), 0)
+        nc.sync.dma_start(out=bias_rows[0:N_GC, :], in_=b_ih0.rearrange("(r c) -> r c", c=P))
+        nc.sync.dma_start(out=bias_rows[N_GC : 2 * N_GC, :], in_=b_hh0.rearrange("(r c) -> r c", c=P))
+        nc.sync.dma_start(
+            out=bias_rows[2 * N_GC : 2 * N_GC + N_JC, :], in_=attn_b.rearrange("(r c) -> r c", c=P)
+        )
+        bias_ps = psum_move.tile([P, P], BF16, tag="move")
+        nc.tensor.transpose(bias_ps[:], bias_rows[:], ident_bf[:])
+        bias_cols = keep.tile([P, P], F32)
+        nc.scalar.copy(out=bias_cols[:], in_=bias_ps[:])
+        attn_bias = bias_cols[:, 2 * N_GC : 2 * N_GC + N_JC]
+        gate_bias = keep.tile([P, N_GC], F32)
+        nc.vector.tensor_tensor(
+            out=gate_bias[:], in0=bias_cols[:, 0:N_GC], in1=bias_cols[:, N_GC : 2 * N_GC], op=ALU.add
+        )
+        for gate in range(N_GATES):
+            cols = slice(gate * N_JC, (gate + 1) * N_JC)
+            nc.vector.tensor_scalar_mul(out=gate_bias[:, cols], in0=gate_bias[:, cols], scalar1=GATE_SCALE[gate])
+
+        def operand_tiles(n_chunks, label):
+            words = keep.tile([P, n_chunks, P], U32, name=label + "_words", align_bytes=64)
+            scales = keep.tile([P, n_chunks, P], U8, name=label + "_scales", align_bytes=64)
+            return words, scales
+
+        x_q = operand_tiles(N_BT, "x")
+        h_q = operand_tiles(N_BT, "h")
+        attn_w_q = operand_tiles(N_JC, "attn_w")
+        w_x_q = operand_tiles(N_GC, "w_x")
+        w_att_q = operand_tiles(N_GC, "w_att")
+        w_h_q = operand_tiles(N_GC, "w_h")
+
+        def bring_k_to_partitions(group):
+            matrix, k_cols, operand, first_chunk, n_chunks = group
+            rows = matrix[first_chunk * P : (first_chunk + n_chunks) * P, k_cols]
+            raw = raw_pool.tile([P, n_chunks, K_PASS], BF16)
+            nc.sync.dma_start(out=raw[:], in_=rows.rearrange("(a r) k -> r a k", r=P))
+            grouped = grouped_pool.tile([P, n_chunks, P, PACK], BF16, align_bytes=64)
+            for a0 in range(0, n_chunks, 2):
+                k_first = psum_move.tile([P, 2, PACK, P], BF16, tag="move")
+                for a in range(2):
+                    for t in range(PACK):
+                        nc.tensor.transpose(k_first[:, a, t, :], raw[:, a0 + a, t:K_PASS:PACK], ident_bf[:])
+                nc.scalar.copy(out=grouped[:, a0 : a0 + 2, :, :], in_=k_first[:].rearrange("p a t r -> p a r t"))
+            return grouped
+
+        def quantise(group, grouped):
+            matrix, k_cols, operand, first_chunk, n_chunks = group
+            words, scales = operand
+            chunks = slice(first_chunk, first_chunk + n_chunks)
+            nc.vector.quantize_mx(
+                out=words[:, chunks, :].rearrange("p a r -> p (a r)").bitcast(FP8X4),
+                scales=scales[:, chunks, :].rearrange("p a r -> p (a r)"),
+                in_=grouped[:].rearrange("p a r t -> p (a r t)"),
+            )
+
+        enc_of, enc_r_of, lin_of, e_of, top_of, enc_e_of = {}, {}, {}, {}, {}, {}
+        e_sum_of, enc_e_sum_of, cell_of = {}, {}, {}
+
+        def load_enc(bt):
+            enc_sb = enc_pool.tile([P, S, H], BF16)
+            nc.sync.dma_start(
+                out=enc_sb[:], in_=enc_seq[:, bt * P : (bt + 1) * P, :].rearrange("s b j -> b s j")
+            )
+            enc_of[bt] = enc_sb
+
+        def attn_lin_into_psum(bt):
+            lin_t_ps = psum_move.tile([P, N_JC, P], F32, tag="move")
+            for jc in range(N_JC):
+                nc.tensor.matmul_mx(
+                    out=lin_t_ps[:, jc, :],
+                    lhsT=attn_w_q[0][:, jc, :].bitcast(FP8X4),
+                    lhsT_scale=attn_w_q[1][:, jc, :],
+                    rhs=x_q[0][:, bt, :].bitcast(FP8X4),
+                    rhs_scale=x_q[1][:, bt, :],
+                    start=True,
+                    stop=True,
+                )
+            lin_t = row_pool.tile([P, N_JC, P], F32)
+            for jc in range(N_JC):
+                nc.scalar.activation(
+                    out=lin_t[:, jc, :], in_=lin_t_ps[:, jc, :], func=FUNC.Identity, bias=attn_bias[:, jc : jc + 1]
+                )
+            lin_ps = psum_lin.tile([P, H], F32)
+            for jc in range(N_JC):
+                nc.tensor.transpose(lin_ps[:, jc * P : (jc + 1) * P], lin_t[:, jc, :], ident_f32[:])
+            lin_of[bt] = lin_ps
+
+        soft_shape = [P, S_OUT, P, S_RUN]
+
+        def over_s(tile_ap):
+            return tile_ap.rearrange("p o j r -> p j o r")
+
+        def for_all_s(row_ap):
+            return row_ap.unsqueeze(1).unsqueeze(3).to_broadcast(soft_shape)
+
+        def regroup_enc(c):
+            bt, jc = divmod(c, N_JC)
+            enc_r = soft_pool.tile(soft_shape, BF16)
+            nc.scalar.copy(
+                out=enc_r[:],
+                in_=enc_of[bt][:, :, jc * P : (jc + 1) * P].rearrange("p (o r) j -> p o j r", r=S_RUN),
+            )
+            enc_r_of[c] = enc_r
+
+        def scores(c):
+            bt, jc = divmod(c, N_JC)
+            e = soft_pool.tile(soft_shape, F32)
+            nc.vector.tensor_tensor(
+                out=e[:], in0=for_all_s(lin_of[bt][:, jc * P : (jc + 1) * P]), in1=enc_r_of[c][:], op=ALU.mult
+            )
+            e_of[c] = e
+
+        def max_over_s(c):
+            top = soft_pool.tile([P, P], F32)
+            nc.vector.tensor_reduce(out=top[:], in_=over_s(e_of[c][:]), axis=INNER_TWO, op=ALU.max)
+            top_of[c] = top
+
+        def subtract_max(c):
+            nc.gpsimd.tensor_tensor(out=e_of[c][:], in0=e_of[c][:], in1=for_all_s(top_of[c][:]), op=ALU.subtract)
+
+        def exponential(c):
+            e_flat = e_of[c][:].rearrange("p o j r -> p (o j r)")
+            nc.scalar.activation(out=e_flat, in_=e_flat, func=FUNC.Exp)
+
+        def weigh_enc(c):
+            enc_e = prod_pool.tile(soft_shape, F32)
+            nc.gpsimd.tensor_tensor(out=enc_e[:], in0=enc_r_of[c][:], in1=e_of[c][:], op=ALU.mult)
+            enc_e_of[c] = enc_e
+
+        def sum_e(c):
+            bt, jc = divmod(c, N_JC)
+            if jc == 0:
+                e_sum = row_pool.tile([P, H], F32)
+                e_sum_of[bt] = e_sum
+            nc.vector.tensor_reduce(
+                out=e_sum_of[bt][:, jc * P : (jc + 1) * P], in_=over_s(e_of[c][:]), axis=INNER_TWO, op=ALU.add
+            )
+
+        def sum_enc_e(c):
+            bt, jc = divmod(c, N_JC)
+            if jc == 0:
+                enc_e_sum = row_pool.tile([P, H], F32)
+                enc_e_sum_of[bt] = enc_e_sum
+            nc.vector.tensor_reduce(
+                out=enc_e_sum_of[bt][:, jc * P : (jc + 1) * P], in_=over_s(enc_e_of[c][:]), axis=INNER_TWO, op=ALU.add
+            )
+
+        def transposed_into_psum(row_tile):
+            t_ps = psum_move.tile([P, PACK, P], F32, tag="move")
+            for t in range(PACK):
+                nc.tensor.transpose(t_ps[:, t, :], row_tile[:, t:H:PACK], ident_f32[:])
+            return t_ps
+
+        def one_over_e_sum(bt):
+            e_sum_t_ps = transposed_into_psum(e_sum_of[bt])
+            inv_t = row_pool.tile([P, PACK, P], F32)
+            nc.scalar.activation(out=inv_t[:], in_=e_sum_t_ps[:], func=FUNC.Ln)
+            nc.scalar.activation(out=inv_t[:], in_=inv_t[:], func=FUNC.Exp, scale=-1.0)
+            cell_of[bt, "inv_t"] = inv_t
+
+        def transpose_enc_e_sum(bt):
+            cell_of[bt, "enc_e_sum_t_ps"] = transposed_into_psum(enc_e_sum_of[bt])
+
+        def attention(bt):
+            att_grouped = row_pool.tile([P, P, PACK], BF16, align_bytes=64)
+            nc.vector.tensor_tensor(
+                out=att_grouped[:],
+                in0=cell_of[bt, "enc_e_sum_t_ps"][:].rearrange("p t b -> p b t"),
+                in1=cell_of[bt, "inv_t"][:].rearrange("p t b -> p b t"),
+                op=ALU.mult,
+            )
+            cell_of[bt, "att_grouped"] = att_grouped
+
+        def load_c(bt):
+            c_raw = row_pool.tile([P, H], BF16)
+            nc.sync.dma_start(out=c_raw[:], in_=c_prev[bt * P : (bt + 1) * P, :])
+            cell_of[bt, "c_raw"] = c_raw
+
+        def quantise_attention(bt):
+            att_words = row_pool.tile([P, P], U32, align_bytes=64)
+            att_scales = row_pool.tile([P, P], U8, align_bytes=64)
+            nc.vector.quantize_mx(
+                out=att_words[:].bitcast(FP8X4),
+                scales=att_scales[:],
+                in_=cell_of[bt, "att_grouped"][:].rearrange("p b t -> p (b t)"),
+            )
+            cell_of[bt, "att_q"] = (att_words, att_scales)
+
+        def gates(bt):
+            att_words, att_scales = cell_of[bt, "att_q"]
+            c_t_ps = psum_move.tile([P, N_JC, P], BF16, tag="move")
+            for jc in range(N_JC):
+                nc.tensor.transpose(c_t_ps[:, jc, :], cell_of[bt, "c_raw"][:, jc * P : (jc + 1) * P], ident_bf[:])
+            products = (
+                (w_x_q, x_q[0][:, bt, :], x_q[1][:, bt, :]),
+                (w_h_q, h_q[0][:, bt, :], h_q[1][:, bt, :]),
+                (w_att_q, att_words[:], att_scales[:]),
+            )
+            tanh_gate = cell_pool.tile([P, N_JC, N_GATES, P], F32)
+            for jc in range(N_JC):
+                gates_ps = psum_gates.tile([P, N_GATES, P], F32)
+                for gate in range(N_GATES):
+                    gc = gate * N_JC + jc
+                    for i, (weights, v_words, v_scales) in enumerate(products):
+                        nc.tensor.matmul_mx(
+                            out=gates_ps[:, gate, :],
+                            lhsT=weights[0][:, gc, :].bitcast(FP8X4),
+                            lhsT_scale=weights[1][:, gc, :],
+                            rhs=v_words.bitcast(FP8X4),
+                            rhs_scale=v_scales,
+                            start=(i == 0),
+                            stop=(i == len(products) - 1),
+                        )
+                for gate in range(N_GATES):
+                    gc = gate * N_JC + jc
+                    nc.scalar.activation(
+                        out=tanh_gate[:, jc, gate, :],
+                        in_=gates_ps[:, gate, :],
+                        func=FUNC.Tanh,
+                        bias=gate_bias[:, gc : gc + 1],
+                        scale=GATE_SCALE[gate],
+                    )
+            nc.scalar.add(out=tanh_gate[:, :, GATE_O, :], in_=tanh_gate[:, :, GATE_O, :], add=1.0)
+            tanh_g_ps = psum_move.tile([P, N_JC, P], F32, tag="move")
+            nc.tensor.matmul(out=tanh_g_ps[:], lhsT=ident_f32[:], rhs=tanh_gate[:, :, GATE_G, :], start=True, stop=True)
+            cell_of[bt, "c_t_ps"] = c_t_ps
+            cell_of[bt, "tanh_g_ps"] = tanh_g_ps
+            cell_of[bt, "tanh_gate"] = tanh_gate
+
+        def kept_and_fresh(bt):
+            tanh_gate = cell_of[bt, "tanh_gate"]
+            kept = cell_pool.tile([P, N_JC, P], F32)
+            nc.vector.scalar_tensor_tensor(
+                out=kept[:],
+                in0=tanh_gate[:, :, GATE_F, :],
+                scalar=1.0,
+                in1=cell_of[bt, "c_t_ps"][:],
+                op0=ALU.add,
+                op1=ALU.mult,
+            )
+            fresh = cell_pool.tile([P, N_JC, P], F32)
+            nc.vector.scalar_tensor_tensor(
+                out=fresh[:],
+                in0=tanh_gate[:, :, GATE_I, :],
+                scalar=1.0,
+                in1=cell_of[bt, "tanh_g_ps"][:],
+                op0=ALU.add,
+                op1=ALU.mult,
+            )
+            cell_of[bt, "kept"] = kept
+            cell_of[bt, "fresh"] = fresh
+
+        def new_state(bt):
+            b_rows = slice(bt * P, (bt + 1) * P)
+            tanh_gate = cell_of[bt, "tanh_gate"]
+            kept = cell_of[bt, "kept"]
+            fresh = cell_of[bt, "fresh"]
+            c_twice_ps = psum_move.tile([P, H], F32, tag="move")
+            for jc in range(N_JC):
+                j_cols = slice(jc * P, (jc + 1) * P)
+                nc.tensor.matmul(out=c_twice_ps[:, j_cols], lhsT=kept[:, jc, :], rhs=ident_f32[:], start=True, stop=False)
+                nc.tensor.matmul(out=c_twice_ps[:, j_cols], lhsT=fresh[:, jc, :], rhs=ident_f32[:], start=False, stop=True)
+            c_new = out_pool.tile([P, H], F32)
+            nc.scalar.mul(out=c_new[:], in_=c_twice_ps[:], mul=0.5)
+            nc.sync.dma_start(out=out_1[b_rows, :], in_=c_new[:])
+            tanh_c = cell_pool.tile([P, H], F32)
+            nc.scalar.activation(out=tanh_c[:], in_=c_twice_ps[:], func=FUNC.Tanh, scale=0.5)
+            o_twice_ps = psum_move.tile([P, H], F32, tag="move")
+            for jc in range(N_JC):
+                nc.tensor.transpose(o_twice_ps[:, jc * P : (jc + 1) * P], tanh_gate[:, jc, GATE_O, :], ident_f32[:])
+            cell_of[bt, "tanh_c"] = tanh_c
+            cell_of[bt, "o_twice_ps"] = o_twice_ps
+
+        def new_output(bt):
+            h_new = out_pool.tile([P, H], F32)
+            nc.vector.scalar_tensor_tensor(
+                out=h_new[:],
+                in0=cell_of[bt, "o_twice_ps"][:],
+                scalar=0.5,
+                in1=cell_of[bt, "tanh_c"][:],
+                op0=ALU.mult,
+                op1=ALU.mult,
+            )
+            nc.sync.dma_start(out=out_0[bt * P : (bt + 1) * P, :], in_=h_new[:])
+
+        first_half = slice(0, H)
+        second_half = slice(H, 2 * H)
+        half_batch = N_BT // 2
+        first = [(x, first_half, x_q, 0, half_batch), (attn_W, first_half, attn_w_q, 0, N_JC)]
+        later = [(x, first_half, x_q, half_batch, half_batch), (h_prev, first_half, h_q, 0, N_BT)]
+        for first_chunk in range(0, N_GC, 8):
+            later += [
+                (W_ih0, first_half, w_x_q, first_chunk, 8),
+                (W_hh0, first_half, w_h_q, first_chunk, 8),
+                (W_ih0, second_half, w_att_q, first_chunk, 8),
+            ]
+        later_grouped = []
+
+        def for_chunk(c, *stages):
+            if 0 <= c < N_CHUNKS:
+                for stage in stages:
+                    stage(c)
+
+        def for_tile(first_chunk, *stages):
+            bt, jc = divmod(first_chunk, N_JC)
+            if jc == 0 and 0 <= bt < N_BT:
+                for stage in stages:
+                    stage(bt)
+
+        with tc.manual_schedule():
+            for group in first:
+                quantise(group, bring_k_to_partitions(group))
+
+            for step in range(-4, N_CHUNKS + 8):
+                for_tile(step + 4, load_enc, attn_lin_into_psum)
+                for_chunk(step + 2, regroup_enc)
+                for_chunk(step + 1, scores, max_over_s)
+                for_tile(step - 7, attention, quantise_attention)
+                if 0 <= step - 1 < len(later):
+                    quantise(later[step - 1], later_grouped[step - 1])
+                for_chunk(step, subtract_max, exponential)
+                for_chunk(step - 1, weigh_enc, sum_e)
+                for_chunk(step - 2, sum_enc_e)
+                for_tile(step - 5, one_over_e_sum, load_c)
+                for_tile(step - 6, transpose_enc_e_sum)
+                for_tile(step - 8, gates)
+                for_tile(step - 9, kept_and_fresh)
+                for_tile(step - 10, new_state)
+                for_tile(step - 11, new_output)
+                if 0 <= step < len(later):
+                    later_grouped.append(bring_k_to_partitions(later[step]))

@@ -16,6 +16,7 @@ INNER_TWO = mybir.AxisListType.XY
 P = 128
 PACK = 4
 K_PASS = P * PACK
+PAIRS = K_PASS // 2
 B, H, S = 1024, 512, 16
 N_BT = B // P
 N_JC = H // P
@@ -23,8 +24,9 @@ N_CHUNKS = N_BT * N_JC
 N_GATES = 4
 GATE_I, GATE_F, GATE_G, GATE_O = 0, 1, 2, 3
 N_GC = N_GATES * N_JC
-S_RUN = 4
+S_RUN = 2
 S_OUT = S // S_RUN
+S_OUT_VECTOR = 4
 GATE_SCALE = (0.5, 0.5, 1.0, 0.5)
 
 FLOPS = 2 * B * H * H + 2 * B * (3 * H) * (N_GATES * H)
@@ -37,21 +39,27 @@ def tile_decoderlstm_pa_t_kernel(
     with ExitStack() as ctx:
         keep = ctx.enter_context(tc.tile_pool(name="keep", bufs=1))
         raw_pool = ctx.enter_context(tc.tile_pool(name="raw", bufs=2))
-        grouped_pool = ctx.enter_context(tc.tile_pool(name="grouped", bufs=3))
+        grouped_pool = ctx.enter_context(tc.tile_pool(name="grouped", bufs=2))
         enc_pool = ctx.enter_context(tc.tile_pool(name="enc", bufs=2))
-        soft_pool = ctx.enter_context(tc.tile_pool(name="soft", bufs=4))
-        prod_pool = ctx.enter_context(tc.tile_pool(name="prod", bufs=2))
+        scores_pool = ctx.enter_context(tc.tile_pool(name="scores", bufs=3))
+        top_pool = ctx.enter_context(tc.tile_pool(name="top", bufs=3))
+        e_pool = ctx.enter_context(tc.tile_pool(name="e", bufs=4))
+        prod_pool = ctx.enter_context(tc.tile_pool(name="prod", bufs=3))
         row_pool = ctx.enter_context(tc.tile_pool(name="row", bufs=2))
         cell_pool = ctx.enter_context(tc.tile_pool(name="cell", bufs=1))
         out_pool = ctx.enter_context(tc.tile_pool(name="out", bufs=2))
-        psum_lin = ctx.enter_context(tc.psum_pool(name="psum_lin", bufs=2))
-        psum_gates = ctx.enter_context(tc.psum_pool(name="psum_gates", bufs=2))
-        psum_move = ctx.enter_context(tc.psum_pool(name="psum_move", bufs=4))
+        psum_row = ctx.enter_context(tc.psum_pool(name="psum_row", bufs=1))
+        psum_sum = ctx.enter_context(tc.psum_pool(name="psum_sum", bufs=1))
+        psum_gates = ctx.enter_context(tc.psum_pool(name="psum_gates", bufs=1))
+        psum_move = ctx.enter_context(tc.psum_pool(name="psum_move", bufs=3))
 
         ident_bf = keep.tile([P, P], BF16)
         make_identity(nc, ident_bf[:])
         ident_f32 = keep.tile([P, P], F32)
         make_identity(nc, ident_f32[:])
+        rows_even_ps = psum_row.tile([P, P], F32)
+        rows_odd_ps = psum_row.tile([P, P], F32)
+        rows_ps = (rows_even_ps, rows_odd_ps)
 
         bias_rows = keep.tile([P, P], BF16)
         nc.vector.memset(bias_rows[:].bitcast(I32), 0)
@@ -90,13 +98,15 @@ def tile_decoderlstm_pa_t_kernel(
             rows = matrix[first_chunk * P : (first_chunk + n_chunks) * P, k_cols]
             raw = raw_pool.tile([P, n_chunks, K_PASS], BF16)
             nc.sync.dma_start(out=raw[:], in_=rows.rearrange("(a r) k -> r a k", r=P))
+            raw_pairs = raw[:].bitcast(F32)
             grouped = grouped_pool.tile([P, n_chunks, P, PACK], BF16, align_bytes=64)
+            grouped_pairs = grouped[:].bitcast(F32)
             for a0 in range(0, n_chunks, 2):
-                k_first = psum_move.tile([P, 2, PACK, P], BF16, tag="move")
+                k_first = psum_move.tile([P, 2, 2, P], F32, tag="move")
                 for a in range(2):
-                    for t in range(PACK):
-                        nc.tensor.transpose(k_first[:, a, t, :], raw[:, a0 + a, t:K_PASS:PACK], ident_bf[:])
-                nc.scalar.copy(out=grouped[:, a0 : a0 + 2, :, :], in_=k_first[:].rearrange("p a t r -> p a r t"))
+                    for u in range(2):
+                        nc.tensor.transpose(k_first[:, a, u, :], raw_pairs[:, a0 + a, u:PAIRS:2], ident_f32[:])
+                nc.scalar.copy(out=grouped_pairs[:, a0 : a0 + 2, :, :], in_=k_first[:].rearrange("p a u r -> p a r u"))
             return grouped
 
         def quantise(group, grouped):
@@ -109,8 +119,8 @@ def tile_decoderlstm_pa_t_kernel(
                 in_=grouped[:].rearrange("p a r t -> p (a r t)"),
             )
 
-        enc_of, enc_r_of, lin_of, e_of, top_of, enc_e_of = {}, {}, {}, {}, {}, {}
-        e_sum_of, enc_e_sum_of, cell_of = {}, {}, {}
+        enc_of, lin_t_of, scores_of, top_of, e_of, enc_e_of = {}, {}, {}, {}, {}, {}
+        sums_of, cell_of = {}, {}
 
         def load_enc(bt):
             enc_sb = enc_pool.tile([P, S, H], BF16)
@@ -119,7 +129,7 @@ def tile_decoderlstm_pa_t_kernel(
             )
             enc_of[bt] = enc_sb
 
-        def attn_lin_into_psum(bt):
+        def attn_lin(bt):
             lin_t_ps = psum_move.tile([P, N_JC, P], F32, tag="move")
             for jc in range(N_JC):
                 nc.tensor.matmul_mx(
@@ -136,95 +146,104 @@ def tile_decoderlstm_pa_t_kernel(
                 nc.scalar.activation(
                     out=lin_t[:, jc, :], in_=lin_t_ps[:, jc, :], func=FUNC.Identity, bias=attn_bias[:, jc : jc + 1]
                 )
-            lin_ps = psum_lin.tile([P, H], F32)
-            for jc in range(N_JC):
-                nc.tensor.transpose(lin_ps[:, jc * P : (jc + 1) * P], lin_t[:, jc, :], ident_f32[:])
-            lin_of[bt] = lin_ps
-
-        soft_shape = [P, S_OUT, P, S_RUN]
+            lin_t_of[bt] = lin_t
 
         def over_s(tile_ap):
             return tile_ap.rearrange("p o j r -> p j o r")
 
-        def for_all_s(row_ap):
-            return row_ap.unsqueeze(1).unsqueeze(3).to_broadcast(soft_shape)
+        def for_s(row_ap, n_out):
+            return row_ap.unsqueeze(1).unsqueeze(3).to_broadcast([P, n_out, P, S_RUN])
 
-        def regroup_enc(c):
+        def lin_into_psum(c):
             bt, jc = divmod(c, N_JC)
-            enc_r = soft_pool.tile(soft_shape, BF16)
-            nc.scalar.copy(
-                out=enc_r[:],
-                in_=enc_of[bt][:, :, jc * P : (jc + 1) * P].rearrange("p (o r) j -> p o j r", r=S_RUN),
-            )
-            enc_r_of[c] = enc_r
+            nc.tensor.transpose(rows_ps[c % 2][:], lin_t_of[bt][:, jc, :], ident_f32[:])
 
         def scores(c):
             bt, jc = divmod(c, N_JC)
-            e = soft_pool.tile(soft_shape, F32)
+            sc = scores_pool.tile([P, S_OUT, P, S_RUN], F32)
             nc.vector.tensor_tensor(
-                out=e[:], in0=for_all_s(lin_of[bt][:, jc * P : (jc + 1) * P]), in1=enc_r_of[c][:], op=ALU.mult
+                out=sc[:],
+                in0=for_s(rows_ps[c % 2][:], S_OUT),
+                in1=enc_of[bt][:, :, jc * P : (jc + 1) * P].rearrange("p (o r) j -> p o j r", r=S_RUN),
+                op=ALU.mult,
+            )
+            scores_of[c] = sc
+
+        def max_over_s(c):
+            top = top_pool.tile([P, P], F32)
+            nc.vector.tensor_reduce(out=top[:], in_=over_s(scores_of[c][:]), axis=INNER_TWO, op=ALU.max)
+            top_of[c] = top
+
+        def max_into_psum(c):
+            nc.tensor.matmul(out=rows_ps[c % 2][:], lhsT=ident_f32[:], rhs=top_of[c][:], start=True, stop=True)
+
+        def subtract_max(c):
+            for_vector = scores_of[c][:, 0:S_OUT_VECTOR, :, :]
+            nc.vector.tensor_tensor(
+                out=for_vector, in0=for_vector, in1=for_s(rows_ps[c % 2][:], S_OUT_VECTOR), op=ALU.subtract
+            )
+            for_gpsimd = scores_of[c][:, S_OUT_VECTOR:S_OUT, :, :]
+            nc.gpsimd.tensor_tensor(
+                out=for_gpsimd, in0=for_gpsimd, in1=for_s(top_of[c][:], S_OUT - S_OUT_VECTOR), op=ALU.subtract
+            )
+
+        def exponential(c):
+            e = e_pool.tile([P, S, P], F32)
+            nc.scalar.activation(
+                out=e[:].rearrange("p (o r) j -> p o j r", r=S_RUN), in_=scores_of[c][:], func=FUNC.Exp
             )
             e_of[c] = e
 
-        def max_over_s(c):
-            top = soft_pool.tile([P, P], F32)
-            nc.vector.tensor_reduce(out=top[:], in_=over_s(e_of[c][:]), axis=INNER_TWO, op=ALU.max)
-            top_of[c] = top
-
-        def subtract_max(c):
-            nc.gpsimd.tensor_tensor(out=e_of[c][:], in0=e_of[c][:], in1=for_all_s(top_of[c][:]), op=ALU.subtract)
-
-        def exponential(c):
-            e_flat = e_of[c][:].rearrange("p o j r -> p (o j r)")
-            nc.scalar.activation(out=e_flat, in_=e_flat, func=FUNC.Exp)
-
         def weigh_enc(c):
-            enc_e = prod_pool.tile(soft_shape, F32)
-            nc.gpsimd.tensor_tensor(out=enc_e[:], in0=enc_r_of[c][:], in1=e_of[c][:], op=ALU.mult)
+            bt, jc = divmod(c, N_JC)
+            enc_e = prod_pool.tile([P, S, P], F32)
+            nc.gpsimd.tensor_tensor(
+                out=enc_e[:], in0=enc_of[bt][:, :, jc * P : (jc + 1) * P], in1=e_of[c][:], op=ALU.mult
+            )
             enc_e_of[c] = enc_e
 
-        def sum_e(c):
+        def sum_over_s(c):
             bt, jc = divmod(c, N_JC)
             if jc == 0:
-                e_sum = row_pool.tile([P, H], F32)
-                e_sum_of[bt] = e_sum
-            nc.vector.tensor_reduce(
-                out=e_sum_of[bt][:, jc * P : (jc + 1) * P], in_=over_s(e_of[c][:]), axis=INNER_TWO, op=ALU.add
-            )
-
-        def sum_enc_e(c):
-            bt, jc = divmod(c, N_JC)
-            if jc == 0:
-                enc_e_sum = row_pool.tile([P, H], F32)
-                enc_e_sum_of[bt] = enc_e_sum
-            nc.vector.tensor_reduce(
-                out=enc_e_sum_of[bt][:, jc * P : (jc + 1) * P], in_=over_s(enc_e_of[c][:]), axis=INNER_TWO, op=ALU.add
-            )
-
-        def transposed_into_psum(row_tile):
-            t_ps = psum_move.tile([P, PACK, P], F32, tag="move")
-            for t in range(PACK):
-                nc.tensor.transpose(t_ps[:, t, :], row_tile[:, t:H:PACK], ident_f32[:])
-            return t_ps
+                e_sum_ps = psum_sum.tile([P, N_JC, P], F32)
+                enc_e_sum_ps = psum_sum.tile([P, N_JC, P], F32)
+                sums_of[bt] = (e_sum_ps, enc_e_sum_ps)
+            for sum_ps, terms in zip(sums_of[bt], (e_of[c], enc_e_of[c])):
+                for s in range(S):
+                    nc.tensor.matmul(
+                        out=sum_ps[:, jc, :],
+                        lhsT=terms[:, s, :],
+                        rhs=ident_f32[:],
+                        is_transpose=True,
+                        start=(s == 0),
+                        stop=(s == S - 1),
+                    )
 
         def one_over_e_sum(bt):
-            e_sum_t_ps = transposed_into_psum(e_sum_of[bt])
-            inv_t = row_pool.tile([P, PACK, P], F32)
-            nc.scalar.activation(out=inv_t[:], in_=e_sum_t_ps[:], func=FUNC.Ln)
+            inv_t = row_pool.tile([P, N_JC, P], F32)
+            nc.scalar.activation(out=inv_t[:], in_=sums_of[bt][0][:], func=FUNC.Ln)
             nc.scalar.activation(out=inv_t[:], in_=inv_t[:], func=FUNC.Exp, scale=-1.0)
             cell_of[bt, "inv_t"] = inv_t
 
-        def transpose_enc_e_sum(bt):
-            cell_of[bt, "enc_e_sum_t_ps"] = transposed_into_psum(enc_e_sum_of[bt])
-
         def attention(bt):
+            att_t = row_pool.tile([P, N_JC, P], BF16)
+            nc.vector.tensor_tensor(out=att_t[:], in0=sums_of[bt][1][:], in1=cell_of[bt, "inv_t"][:], op=ALU.mult)
+            cell_of[bt, "att_t"] = att_t
+
+        def attention_rows(bt):
+            att_ps = psum_move.tile([P, H], BF16, tag="move")
+            for jc in range(N_JC):
+                nc.tensor.transpose(att_ps[:, jc * P : (jc + 1) * P], cell_of[bt, "att_t"][:, jc, :], ident_bf[:])
+            att = row_pool.tile([P, H], BF16)
+            nc.scalar.copy(out=att[:], in_=att_ps[:])
+            cell_of[bt, "att"] = att
+
+        def group_attention(bt):
+            att_k_ps = psum_move.tile([P, PACK, P], BF16, tag="move")
+            for t in range(PACK):
+                nc.tensor.transpose(att_k_ps[:, t, :], cell_of[bt, "att"][:, t:H:PACK], ident_bf[:])
             att_grouped = row_pool.tile([P, P, PACK], BF16, align_bytes=64)
-            nc.vector.tensor_tensor(
-                out=att_grouped[:],
-                in0=cell_of[bt, "enc_e_sum_t_ps"][:].rearrange("p t b -> p b t"),
-                in1=cell_of[bt, "inv_t"][:].rearrange("p t b -> p b t"),
-                op=ALU.mult,
-            )
+            nc.scalar.copy(out=att_grouped[:], in_=att_k_ps[:].rearrange("p t b -> p b t"))
             cell_of[bt, "att_grouped"] = att_grouped
 
         def load_c(bt):
@@ -242,46 +261,49 @@ def tile_decoderlstm_pa_t_kernel(
             )
             cell_of[bt, "att_q"] = (att_words, att_scales)
 
-        def gates(bt):
+        def gates(bt, jc):
             att_words, att_scales = cell_of[bt, "att_q"]
-            c_t_ps = psum_move.tile([P, N_JC, P], BF16, tag="move")
-            for jc in range(N_JC):
-                nc.tensor.transpose(c_t_ps[:, jc, :], cell_of[bt, "c_raw"][:, jc * P : (jc + 1) * P], ident_bf[:])
             products = (
                 (w_x_q, x_q[0][:, bt, :], x_q[1][:, bt, :]),
                 (w_h_q, h_q[0][:, bt, :], h_q[1][:, bt, :]),
                 (w_att_q, att_words[:], att_scales[:]),
             )
-            tanh_gate = cell_pool.tile([P, N_JC, N_GATES, P], F32)
-            for jc in range(N_JC):
-                gates_ps = psum_gates.tile([P, N_GATES, P], F32)
-                for gate in range(N_GATES):
-                    gc = gate * N_JC + jc
-                    for i, (weights, v_words, v_scales) in enumerate(products):
-                        nc.tensor.matmul_mx(
-                            out=gates_ps[:, gate, :],
-                            lhsT=weights[0][:, gc, :].bitcast(FP8X4),
-                            lhsT_scale=weights[1][:, gc, :],
-                            rhs=v_words.bitcast(FP8X4),
-                            rhs_scale=v_scales,
-                            start=(i == 0),
-                            stop=(i == len(products) - 1),
-                        )
-                for gate in range(N_GATES):
-                    gc = gate * N_JC + jc
-                    nc.scalar.activation(
-                        out=tanh_gate[:, jc, gate, :],
-                        in_=gates_ps[:, gate, :],
-                        func=FUNC.Tanh,
-                        bias=gate_bias[:, gc : gc + 1],
-                        scale=GATE_SCALE[gate],
+            if jc == 0:
+                tanh_gate = row_pool.tile([P, N_JC, N_GATES, P], F32)
+                cell_of[bt, "tanh_gate"] = tanh_gate
+            gates_ps = psum_gates.tile([P, N_GATES, P], F32)
+            for gate in range(N_GATES):
+                gc = gate * N_JC + jc
+                for i, (weights, v_words, v_scales) in enumerate(products):
+                    nc.tensor.matmul_mx(
+                        out=gates_ps[:, gate, :],
+                        lhsT=weights[0][:, gc, :].bitcast(FP8X4),
+                        lhsT_scale=weights[1][:, gc, :],
+                        rhs=v_words.bitcast(FP8X4),
+                        rhs_scale=v_scales,
+                        start=(i == 0),
+                        stop=(i == len(products) - 1),
                     )
-            nc.scalar.add(out=tanh_gate[:, :, GATE_O, :], in_=tanh_gate[:, :, GATE_O, :], add=1.0)
+            for gate in range(N_GATES):
+                gc = gate * N_JC + jc
+                nc.scalar.activation(
+                    out=cell_of[bt, "tanh_gate"][:, jc, gate, :],
+                    in_=gates_ps[:, gate, :],
+                    func=FUNC.Tanh,
+                    bias=gate_bias[:, gc : gc + 1],
+                    scale=GATE_SCALE[gate],
+                )
+
+        def cell_inputs(bt):
+            tanh_gate = cell_of[bt, "tanh_gate"]
+            c_t_ps = psum_move.tile([P, N_JC, P], BF16, tag="move")
+            for jc in range(N_JC):
+                nc.tensor.transpose(c_t_ps[:, jc, :], cell_of[bt, "c_raw"][:, jc * P : (jc + 1) * P], ident_bf[:])
             tanh_g_ps = psum_move.tile([P, N_JC, P], F32, tag="move")
             nc.tensor.matmul(out=tanh_g_ps[:], lhsT=ident_f32[:], rhs=tanh_gate[:, :, GATE_G, :], start=True, stop=True)
+            nc.scalar.add(out=tanh_gate[:, :, GATE_O, :], in_=tanh_gate[:, :, GATE_O, :], add=1.0)
             cell_of[bt, "c_t_ps"] = c_t_ps
             cell_of[bt, "tanh_g_ps"] = tanh_g_ps
-            cell_of[bt, "tanh_gate"] = tanh_gate
 
         def kept_and_fresh(bt):
             tanh_gate = cell_of[bt, "tanh_gate"]
@@ -308,14 +330,17 @@ def tile_decoderlstm_pa_t_kernel(
 
         def new_state(bt):
             b_rows = slice(bt * P, (bt + 1) * P)
-            tanh_gate = cell_of[bt, "tanh_gate"]
-            kept = cell_of[bt, "kept"]
-            fresh = cell_of[bt, "fresh"]
             c_twice_ps = psum_move.tile([P, H], F32, tag="move")
             for jc in range(N_JC):
-                j_cols = slice(jc * P, (jc + 1) * P)
-                nc.tensor.matmul(out=c_twice_ps[:, j_cols], lhsT=kept[:, jc, :], rhs=ident_f32[:], start=True, stop=False)
-                nc.tensor.matmul(out=c_twice_ps[:, j_cols], lhsT=fresh[:, jc, :], rhs=ident_f32[:], start=False, stop=True)
+                for i, term in enumerate((cell_of[bt, "kept"], cell_of[bt, "fresh"])):
+                    nc.tensor.matmul(
+                        out=c_twice_ps[:, jc * P : (jc + 1) * P],
+                        lhsT=term[:, jc, :],
+                        rhs=ident_f32[:],
+                        is_transpose=True,
+                        start=(i == 0),
+                        stop=(i == 1),
+                    )
             c_new = out_pool.tile([P, H], F32)
             nc.scalar.mul(out=c_new[:], in_=c_twice_ps[:], mul=0.5)
             nc.sync.dma_start(out=out_1[b_rows, :], in_=c_new[:])
@@ -323,7 +348,9 @@ def tile_decoderlstm_pa_t_kernel(
             nc.scalar.activation(out=tanh_c[:], in_=c_twice_ps[:], func=FUNC.Tanh, scale=0.5)
             o_twice_ps = psum_move.tile([P, H], F32, tag="move")
             for jc in range(N_JC):
-                nc.tensor.transpose(o_twice_ps[:, jc * P : (jc + 1) * P], tanh_gate[:, jc, GATE_O, :], ident_f32[:])
+                nc.tensor.transpose(
+                    o_twice_ps[:, jc * P : (jc + 1) * P], cell_of[bt, "tanh_gate"][:, jc, GATE_O, :], ident_f32[:]
+                )
             cell_of[bt, "tanh_c"] = tanh_c
             cell_of[bt, "o_twice_ps"] = o_twice_ps
 
@@ -367,21 +394,28 @@ def tile_decoderlstm_pa_t_kernel(
             for group in first:
                 quantise(group, bring_k_to_partitions(group))
 
-            for step in range(-4, N_CHUNKS + 8):
-                for_tile(step + 4, load_enc, attn_lin_into_psum)
-                for_chunk(step + 2, regroup_enc)
-                for_chunk(step + 1, scores, max_over_s)
-                for_tile(step - 7, attention, quantise_attention)
+            for step in range(-4, N_CHUNKS + 10):
+                for_tile(step - 12, kept_and_fresh)
+                for_tile(step - 13, new_output)
+                for_tile(step - 6, one_over_e_sum)
+                for_chunk(step, max_into_psum)
+                for_tile(step - 7, group_attention)
+                for_chunk(step + 1, scores)
+                for_chunk(step, subtract_max)
+                for_tile(step - 6, attention)
+                for_chunk(step + 1, max_over_s)
+                for_tile(step - 7, quantise_attention)
                 if 0 <= step - 1 < len(later):
                     quantise(later[step - 1], later_grouped[step - 1])
-                for_chunk(step, subtract_max, exponential)
-                for_chunk(step - 1, weigh_enc, sum_e)
-                for_chunk(step - 2, sum_enc_e)
-                for_tile(step - 5, one_over_e_sum, load_c)
-                for_tile(step - 6, transpose_enc_e_sum)
-                for_tile(step - 8, gates)
-                for_tile(step - 9, kept_and_fresh)
-                for_tile(step - 10, new_state)
-                for_tile(step - 11, new_output)
+                for_chunk(step - 1, weigh_enc)
                 if 0 <= step < len(later):
                     later_grouped.append(bring_k_to_partitions(later[step]))
+                for jc in range(N_JC):
+                    for_tile(step - 8 - jc, lambda bt, jc=jc: gates(bt, jc))
+                for_chunk(step + 2, lin_into_psum)
+                for_chunk(step, exponential)
+                for_chunk(step - 2, sum_over_s)
+                for_tile(step - 6, attention_rows, load_c)
+                for_tile(step + 4, load_enc, attn_lin)
+                for_tile(step - 12, new_state)
+                for_tile(step - 11, cell_inputs)

@@ -46,11 +46,12 @@ def tile_decoderlstm_pa_t_kernel(
         e_pool = ctx.enter_context(tc.tile_pool(name="e", bufs=4))
         prod_pool = ctx.enter_context(tc.tile_pool(name="prod", bufs=3))
         row_pool = ctx.enter_context(tc.tile_pool(name="row", bufs=2))
+        att_pool = ctx.enter_context(tc.tile_pool(name="att", bufs=4))
         cell_pool = ctx.enter_context(tc.tile_pool(name="cell", bufs=1))
         out_pool = ctx.enter_context(tc.tile_pool(name="out", bufs=2))
         psum_row = ctx.enter_context(tc.psum_pool(name="psum_row", bufs=1))
-        psum_sum = ctx.enter_context(tc.psum_pool(name="psum_sum", bufs=1))
-        psum_gates = ctx.enter_context(tc.psum_pool(name="psum_gates", bufs=1))
+        psum_e_sum = ctx.enter_context(tc.psum_pool(name="psum_e_sum", bufs=1))
+        psum_enc_e_sum = ctx.enter_context(tc.psum_pool(name="psum_enc_e_sum", bufs=2))
         psum_move = ctx.enter_context(tc.psum_pool(name="psum_move", bufs=3))
 
         ident_bf = keep.tile([P, P], BF16)
@@ -189,9 +190,12 @@ def tile_decoderlstm_pa_t_kernel(
 
         def exponential(c):
             e = e_pool.tile([P, S, P], F32)
-            nc.scalar.activation(
-                out=e[:].rearrange("p (o r) j -> p o j r", r=S_RUN), in_=scores_of[c][:], func=FUNC.Exp
-            )
+            for o_range in (slice(S_OUT_VECTOR, S_OUT), slice(0, S_OUT_VECTOR)):
+                nc.scalar.activation(
+                    out=e[:].rearrange("p (o r) j -> p o j r", r=S_RUN)[:, o_range, :, :],
+                    in_=scores_of[c][:, o_range, :, :],
+                    func=FUNC.Exp,
+                )
             e_of[c] = e
 
         def weigh_enc(c):
@@ -205,8 +209,8 @@ def tile_decoderlstm_pa_t_kernel(
         def sum_over_s(c):
             bt, jc = divmod(c, N_JC)
             if jc == 0:
-                e_sum_ps = psum_sum.tile([P, N_JC, P], F32)
-                enc_e_sum_ps = psum_sum.tile([P, N_JC, P], F32)
+                e_sum_ps = psum_e_sum.tile([P, N_JC, P], F32)
+                enc_e_sum_ps = psum_enc_e_sum.tile([P, N_JC, P], F32)
                 sums_of[bt] = (e_sum_ps, enc_e_sum_ps)
             for sum_ps, terms in zip(sums_of[bt], (e_of[c], enc_e_of[c])):
                 for s in range(S):
@@ -219,11 +223,14 @@ def tile_decoderlstm_pa_t_kernel(
                         stop=(s == S - 1),
                     )
 
-        def one_over_e_sum(bt):
+        def log_of_e_sum(bt):
             inv_t = row_pool.tile([P, N_JC, P], F32)
             nc.scalar.activation(out=inv_t[:], in_=sums_of[bt][0][:], func=FUNC.Ln)
-            nc.scalar.activation(out=inv_t[:], in_=inv_t[:], func=FUNC.Exp, scale=-1.0)
             cell_of[bt, "inv_t"] = inv_t
+
+        def one_over_e_sum(bt):
+            inv_t = cell_of[bt, "inv_t"]
+            nc.scalar.activation(out=inv_t[:], in_=inv_t[:], func=FUNC.Exp, scale=-1.0)
 
         def attention(bt):
             att_t = row_pool.tile([P, N_JC, P], BF16)
@@ -252,8 +259,8 @@ def tile_decoderlstm_pa_t_kernel(
             cell_of[bt, "c_raw"] = c_raw
 
         def quantise_attention(bt):
-            att_words = row_pool.tile([P, P], U32, align_bytes=64)
-            att_scales = row_pool.tile([P, P], U8, align_bytes=64)
+            att_words = att_pool.tile([P, P], U32, align_bytes=64)
+            att_scales = att_pool.tile([P, P], U8, align_bytes=64)
             nc.vector.quantize_mx(
                 out=att_words[:].bitcast(FP8X4),
                 scales=att_scales[:],
@@ -271,7 +278,7 @@ def tile_decoderlstm_pa_t_kernel(
             if jc == 0:
                 tanh_gate = row_pool.tile([P, N_JC, N_GATES, P], F32)
                 cell_of[bt, "tanh_gate"] = tanh_gate
-            gates_ps = psum_gates.tile([P, N_GATES, P], F32)
+            gates_ps = psum_move.tile([P, N_GATES, P], F32, tag="move")
             for gate in range(N_GATES):
                 gc = gate * N_JC + jc
                 for i, (weights, v_words, v_scales) in enumerate(products):
@@ -370,14 +377,21 @@ def tile_decoderlstm_pa_t_kernel(
         second_half = slice(H, 2 * H)
         half_batch = N_BT // 2
         first = [(x, first_half, x_q, 0, half_batch), (attn_W, first_half, attn_w_q, 0, N_JC)]
-        later = [(x, first_half, x_q, half_batch, half_batch), (h_prev, first_half, h_q, 0, N_BT)]
-        for first_chunk in range(0, N_GC, 8):
+        later = [(x, first_half, x_q, half_batch, half_batch)]
+        for first_chunk in range(0, N_BT, 4):
+            later.append((h_prev, first_half, h_q, first_chunk, 4))
+        for first_chunk in range(0, N_GC, 4):
             later += [
-                (W_ih0, first_half, w_x_q, first_chunk, 8),
-                (W_hh0, first_half, w_h_q, first_chunk, 8),
-                (W_ih0, second_half, w_att_q, first_chunk, 8),
+                (W_ih0, first_half, w_x_q, first_chunk, 4),
+                (W_hh0, first_half, w_h_q, first_chunk, 4),
+                (W_ih0, second_half, w_att_q, first_chunk, 4),
             ]
         later_grouped = []
+
+        first_gate_step = len(later) + 1
+
+        def gate_step(n):
+            return max(n + 8, first_gate_step + n // 2)
 
         def for_chunk(c, *stages):
             if 0 <= c < N_CHUNKS:
@@ -390,32 +404,42 @@ def tile_decoderlstm_pa_t_kernel(
                 for stage in stages:
                     stage(bt)
 
+        def for_gated_tile(step, *stages):
+            for bt in range(N_BT):
+                if gate_step(bt * N_JC + N_JC - 1) == step:
+                    for stage in stages:
+                        stage(bt)
+
         with tc.manual_schedule():
             for group in first:
                 quantise(group, bring_k_to_partitions(group))
 
             for step in range(-4, N_CHUNKS + 10):
-                for_tile(step - 12, kept_and_fresh)
-                for_tile(step - 13, new_output)
+                for_gated_tile(step - 1, kept_and_fresh)
+                for_gated_tile(step - 2, new_output)
                 for_tile(step - 6, one_over_e_sum)
                 for_chunk(step, max_into_psum)
-                for_tile(step - 7, group_attention)
                 for_chunk(step + 1, scores)
                 for_chunk(step, subtract_max)
                 for_tile(step - 6, attention)
                 for_chunk(step + 1, max_over_s)
-                for_tile(step - 7, quantise_attention)
+                for_chunk(step, exponential)
+                for_chunk(step - 2, sum_over_s)
+                for_chunk(step + 2, lin_into_psum)
+                for_tile(step - 7, group_attention, quantise_attention)
                 if 0 <= step - 1 < len(later):
                     quantise(later[step - 1], later_grouped[step - 1])
                 for_chunk(step - 1, weigh_enc)
+                for n in range(N_CHUNKS):
+                    bt, jc = divmod(n, N_JC)
+                    if gate_step(n) == step:
+                        if jc == 0:
+                            load_c(bt)
+                        gates(bt, jc)
                 if 0 <= step < len(later):
                     later_grouped.append(bring_k_to_partitions(later[step]))
-                for jc in range(N_JC):
-                    for_tile(step - 8 - jc, lambda bt, jc=jc: gates(bt, jc))
-                for_chunk(step + 2, lin_into_psum)
-                for_chunk(step, exponential)
-                for_chunk(step - 2, sum_over_s)
-                for_tile(step - 6, attention_rows, load_c)
+                for_tile(step - 6, attention_rows)
+                for_tile(step - 5, log_of_e_sum)
                 for_tile(step + 4, load_enc, attn_lin)
-                for_tile(step - 12, new_state)
-                for_tile(step - 11, cell_inputs)
+                for_gated_tile(step - 1, new_state)
+                for_gated_tile(step, cell_inputs)

@@ -27,6 +27,11 @@ N_GC = N_GATES * N_JC
 S_RUN = 2
 S_OUT = S // S_RUN
 S_OUT_VECTOR = 4
+JC_PER_BANK = N_JC // 2
+N_RUNS = 3
+RUN = -(-2 * S // N_RUNS)
+QUOTA = (2048, 1024, 0)
+PASS_COLUMNS = 128
 GATE_SCALE = (0.5, 0.5, 1.0, 0.5)
 
 FLOPS = 2 * B * H * H + 2 * B * (3 * H) * (N_GATES * H)
@@ -38,8 +43,8 @@ def tile_decoderlstm_pa_t_kernel(
     nc = tc.nc
     with ExitStack() as ctx:
         keep = ctx.enter_context(tc.tile_pool(name="keep", bufs=1))
-        raw_pool = ctx.enter_context(tc.tile_pool(name="raw", bufs=2))
-        grouped_pool = ctx.enter_context(tc.tile_pool(name="grouped", bufs=2))
+        raw_pool = ctx.enter_context(tc.tile_pool(name="raw", bufs=4))
+        grouped_pool = ctx.enter_context(tc.tile_pool(name="grouped", bufs=3))
         enc_pool = ctx.enter_context(tc.tile_pool(name="enc", bufs=2))
         scores_pool = ctx.enter_context(tc.tile_pool(name="scores", bufs=3))
         top_pool = ctx.enter_context(tc.tile_pool(name="top", bufs=3))
@@ -47,20 +52,28 @@ def tile_decoderlstm_pa_t_kernel(
         prod_pool = ctx.enter_context(tc.tile_pool(name="prod", bufs=3))
         row_pool = ctx.enter_context(tc.tile_pool(name="row", bufs=2))
         att_pool = ctx.enter_context(tc.tile_pool(name="att", bufs=4))
-        cell_pool = ctx.enter_context(tc.tile_pool(name="cell", bufs=1))
+        cell_pool = ctx.enter_context(tc.tile_pool(name="cell", bufs=2))
         out_pool = ctx.enter_context(tc.tile_pool(name="out", bufs=2))
         psum_row = ctx.enter_context(tc.psum_pool(name="psum_row", bufs=1))
-        psum_e_sum = ctx.enter_context(tc.psum_pool(name="psum_e_sum", bufs=1))
-        psum_enc_e_sum = ctx.enter_context(tc.psum_pool(name="psum_enc_e_sum", bufs=2))
+        psum_sums = ctx.enter_context(tc.psum_pool(name="psum_sums", bufs=3))
         psum_move = ctx.enter_context(tc.psum_pool(name="psum_move", bufs=3))
 
         ident_bf = keep.tile([P, P], BF16)
         make_identity(nc, ident_bf[:])
         ident_f32 = keep.tile([P, P], F32)
         make_identity(nc, ident_f32[:])
-        rows_even_ps = psum_row.tile([P, P], F32)
-        rows_odd_ps = psum_row.tile([P, P], F32)
-        rows_ps = (rows_even_ps, rows_odd_ps)
+        rows_even_ps = psum_row.tile([P, 3, P], F32)
+        rows_odd_ps = psum_row.tile([P, 3, P], F32)
+        both_rows_ps = (rows_even_ps, rows_odd_ps)
+
+        def row_ps(c):
+            return both_rows_ps[c % 2][:, 0, :]
+
+        def tanh_g_ps(step):
+            return both_rows_ps[step % 2][:, 1, :]
+
+        def c_t_ps(step):
+            return both_rows_ps[step % 2][:, 2, :].bitcast(BF16)[:, 0:P]
 
         bias_rows = keep.tile([P, P], BF16)
         nc.vector.memset(bias_rows[:].bitcast(I32), 0)
@@ -94,11 +107,14 @@ def tile_decoderlstm_pa_t_kernel(
         w_att_q = operand_tiles(N_GC, "w_att")
         w_h_q = operand_tiles(N_GC, "w_h")
 
-        def bring_k_to_partitions(group):
+        def load_rows(group):
             matrix, k_cols, operand, first_chunk, n_chunks = group
             rows = matrix[first_chunk * P : (first_chunk + n_chunks) * P, k_cols]
             raw = raw_pool.tile([P, n_chunks, K_PASS], BF16)
             nc.sync.dma_start(out=raw[:], in_=rows.rearrange("(a r) k -> r a k", r=P))
+            return raw
+
+        def bring_k_to_partitions(raw, n_chunks):
             raw_pairs = raw[:].bitcast(F32)
             grouped = grouped_pool.tile([P, n_chunks, P, PACK], BF16, align_bytes=64)
             grouped_pairs = grouped[:].bitcast(F32)
@@ -121,7 +137,7 @@ def tile_decoderlstm_pa_t_kernel(
             )
 
         enc_of, lin_t_of, scores_of, top_of, e_of, enc_e_of = {}, {}, {}, {}, {}, {}
-        sums_of, cell_of = {}, {}
+        sums_of, gates_of, cell_of, terms_of = {}, {}, {}, {}
 
         def load_enc(bt):
             enc_sb = enc_pool.tile([P, S, H], BF16)
@@ -157,14 +173,14 @@ def tile_decoderlstm_pa_t_kernel(
 
         def lin_into_psum(c):
             bt, jc = divmod(c, N_JC)
-            nc.tensor.transpose(rows_ps[c % 2][:], lin_t_of[bt][:, jc, :], ident_f32[:])
+            nc.tensor.matmul(out=row_ps(c), lhsT=lin_t_of[bt][:, jc, :], rhs=ident_f32[:], start=True, stop=True)
 
         def scores(c):
             bt, jc = divmod(c, N_JC)
             sc = scores_pool.tile([P, S_OUT, P, S_RUN], F32)
             nc.vector.tensor_tensor(
                 out=sc[:],
-                in0=for_s(rows_ps[c % 2][:], S_OUT),
+                in0=for_s(row_ps(c), S_OUT),
                 in1=enc_of[bt][:, :, jc * P : (jc + 1) * P].rearrange("p (o r) j -> p o j r", r=S_RUN),
                 op=ALU.mult,
             )
@@ -176,12 +192,12 @@ def tile_decoderlstm_pa_t_kernel(
             top_of[c] = top
 
         def max_into_psum(c):
-            nc.tensor.matmul(out=rows_ps[c % 2][:], lhsT=ident_f32[:], rhs=top_of[c][:], start=True, stop=True)
+            nc.tensor.matmul(out=row_ps(c), lhsT=ident_f32[:], rhs=top_of[c][:], start=True, stop=True)
 
         def subtract_max(c):
             for_vector = scores_of[c][:, 0:S_OUT_VECTOR, :, :]
             nc.vector.tensor_tensor(
-                out=for_vector, in0=for_vector, in1=for_s(rows_ps[c % 2][:], S_OUT_VECTOR), op=ALU.subtract
+                out=for_vector, in0=for_vector, in1=for_s(row_ps(c), S_OUT_VECTOR), op=ALU.subtract
             )
             for_gpsimd = scores_of[c][:, S_OUT_VECTOR:S_OUT, :, :]
             nc.gpsimd.tensor_tensor(
@@ -206,26 +222,40 @@ def tile_decoderlstm_pa_t_kernel(
             )
             enc_e_of[c] = enc_e
 
-        def sum_over_s(c):
-            bt, jc = divmod(c, N_JC)
-            if jc == 0:
-                e_sum_ps = psum_e_sum.tile([P, N_JC, P], F32)
-                enc_e_sum_ps = psum_enc_e_sum.tile([P, N_JC, P], F32)
-                sums_of[bt] = (e_sum_ps, enc_e_sum_ps)
-            for sum_ps, terms in zip(sums_of[bt], (e_of[c], enc_e_of[c])):
-                for s in range(S):
-                    nc.tensor.matmul(
-                        out=sum_ps[:, jc, :],
-                        lhsT=terms[:, s, :],
-                        rhs=ident_f32[:],
-                        is_transpose=True,
-                        start=(s == 0),
-                        stop=(s == S - 1),
-                    )
+        def idle_pass(out):
+            nc.tensor.matmul_mx(
+                out=out,
+                lhsT=attn_w_q[0][:, 0, :].bitcast(FP8X4),
+                lhsT_scale=attn_w_q[1][:, 0, :],
+                rhs=x_q[0][:, 0, :].bitcast(FP8X4),
+                rhs_scale=x_q[1][:, 0, :],
+                start=True,
+                stop=True,
+            )
+
+        def sum_over_s(c, run):
+            if c % JC_PER_BANK == 0 and run == 0:
+                sums_ps = psum_sums.tile([P, 2, JC_PER_BANK, P], F32)
+                sums_of[c // JC_PER_BANK] = sums_ps
+            sums_ps = sums_of[c // JC_PER_BANK]
+            terms = [(i, tile, s) for i, tile in enumerate((e_of[c], enc_e_of[c])) for s in range(S)]
+            for i, tile, s in terms[run * RUN : (run + 1) * RUN]:
+                nc.tensor.matmul(
+                    out=sums_ps[:, i, c % JC_PER_BANK, :],
+                    lhsT=tile[:, s, :],
+                    rhs=ident_f32[:],
+                    is_transpose=True,
+                    start=(s == 0),
+                    stop=(s == S - 1),
+                )
+
+        def chunks_of(half):
+            return slice(half * JC_PER_BANK, (half + 1) * JC_PER_BANK)
 
         def log_of_e_sum(bt):
             inv_t = row_pool.tile([P, N_JC, P], F32)
-            nc.scalar.activation(out=inv_t[:], in_=sums_of[bt][0][:], func=FUNC.Ln)
+            for half in range(2):
+                nc.scalar.activation(out=inv_t[:, chunks_of(half), :], in_=sums_of[2 * bt + half][:, 0, :, :], func=FUNC.Ln)
             cell_of[bt, "inv_t"] = inv_t
 
         def one_over_e_sum(bt):
@@ -234,7 +264,13 @@ def tile_decoderlstm_pa_t_kernel(
 
         def attention(bt):
             att_t = row_pool.tile([P, N_JC, P], BF16)
-            nc.vector.tensor_tensor(out=att_t[:], in0=sums_of[bt][1][:], in1=cell_of[bt, "inv_t"][:], op=ALU.mult)
+            for half in range(2):
+                nc.vector.tensor_tensor(
+                    out=att_t[:, chunks_of(half), :],
+                    in0=sums_of[2 * bt + half][:, 1, :, :],
+                    in1=cell_of[bt, "inv_t"][:, chunks_of(half), :],
+                    op=ALU.mult,
+                )
             cell_of[bt, "att_t"] = att_t
 
         def attention_rows(bt):
@@ -268,110 +304,122 @@ def tile_decoderlstm_pa_t_kernel(
             )
             cell_of[bt, "att_q"] = (att_words, att_scales)
 
-        def gates(bt, jc):
+        def open_gates(n):
+            gates_ps = psum_move.tile([P, N_GATES, P], F32, tag="move")
+            gates_of[n] = gates_ps
+
+        def gate_product(n, gate):
+            bt, jc = divmod(n, N_JC)
             att_words, att_scales = cell_of[bt, "att_q"]
             products = (
                 (w_x_q, x_q[0][:, bt, :], x_q[1][:, bt, :]),
                 (w_h_q, h_q[0][:, bt, :], h_q[1][:, bt, :]),
                 (w_att_q, att_words[:], att_scales[:]),
             )
+            gc = gate * N_JC + jc
+            for i, (weights, v_words, v_scales) in enumerate(products):
+                nc.tensor.matmul_mx(
+                    out=gates_of[n][:, gate, :],
+                    lhsT=weights[0][:, gc, :].bitcast(FP8X4),
+                    lhsT_scale=weights[1][:, gc, :],
+                    rhs=v_words.bitcast(FP8X4),
+                    rhs_scale=v_scales,
+                    start=(i == 0),
+                    stop=(i == len(products) - 1),
+                )
+
+        def tanh_of_gates(n):
+            bt, jc = divmod(n, N_JC)
             if jc == 0:
-                tanh_gate = row_pool.tile([P, N_JC, N_GATES, P], F32)
-                cell_of[bt, "tanh_gate"] = tanh_gate
-            gates_ps = psum_move.tile([P, N_GATES, P], F32, tag="move")
-            for gate in range(N_GATES):
-                gc = gate * N_JC + jc
-                for i, (weights, v_words, v_scales) in enumerate(products):
-                    nc.tensor.matmul_mx(
-                        out=gates_ps[:, gate, :],
-                        lhsT=weights[0][:, gc, :].bitcast(FP8X4),
-                        lhsT_scale=weights[1][:, gc, :],
-                        rhs=v_words.bitcast(FP8X4),
-                        rhs_scale=v_scales,
-                        start=(i == 0),
-                        stop=(i == len(products) - 1),
-                    )
+                cell_of[bt, "tanh"] = [row_pool.tile([P, N_JC, P], F32, name="tanh_" + label) for label in "ifgo"]
+            gates_ps = gates_of[n]
             for gate in range(N_GATES):
                 gc = gate * N_JC + jc
                 nc.scalar.activation(
-                    out=cell_of[bt, "tanh_gate"][:, jc, gate, :],
+                    out=cell_of[bt, "tanh"][gate][:, jc, :],
                     in_=gates_ps[:, gate, :],
                     func=FUNC.Tanh,
                     bias=gate_bias[:, gc : gc + 1],
                     scale=GATE_SCALE[gate],
                 )
+            tanh_o = cell_of[bt, "tanh"][GATE_O][:, jc, :]
+            nc.scalar.add(out=tanh_o, in_=tanh_o, add=1.0)
 
-        def cell_inputs(bt):
-            tanh_gate = cell_of[bt, "tanh_gate"]
-            c_t_ps = psum_move.tile([P, N_JC, P], BF16, tag="move")
-            for jc in range(N_JC):
-                nc.tensor.transpose(c_t_ps[:, jc, :], cell_of[bt, "c_raw"][:, jc * P : (jc + 1) * P], ident_bf[:])
-            tanh_g_ps = psum_move.tile([P, N_JC, P], F32, tag="move")
-            nc.tensor.matmul(out=tanh_g_ps[:], lhsT=ident_f32[:], rhs=tanh_gate[:, :, GATE_G, :], start=True, stop=True)
-            nc.scalar.add(out=tanh_gate[:, :, GATE_O, :], in_=tanh_gate[:, :, GATE_O, :], add=1.0)
-            cell_of[bt, "c_t_ps"] = c_t_ps
-            cell_of[bt, "tanh_g_ps"] = tanh_g_ps
+        def cell_inputs(n, step):
+            bt, jc = divmod(n, N_JC)
+            nc.tensor.matmul(
+                out=tanh_g_ps(step),
+                lhsT=ident_f32[:],
+                rhs=cell_of[bt, "tanh"][GATE_G][:, jc, :],
+                start=True,
+                stop=True,
+            )
 
-        def kept_and_fresh(bt):
-            tanh_gate = cell_of[bt, "tanh_gate"]
-            kept = cell_pool.tile([P, N_JC, P], F32)
+        def transpose_c(n, step):
+            bt, jc = divmod(n, N_JC)
+            nc.tensor.transpose(c_t_ps(step), cell_of[bt, "c_raw"][:, jc * P : (jc + 1) * P], ident_bf[:])
+
+        def transpose_state(n):
+            bt, jc = divmod(n, N_JC)
+            state_ps = psum_move.tile([P, 2, P], F32, tag="move")
+            for i, term in enumerate(terms_of[n]):
+                nc.tensor.matmul(
+                    out=state_ps[:, 0, :], lhsT=term[:], rhs=ident_f32[:], is_transpose=True, start=(i == 0), stop=(i == 1)
+                )
+            nc.tensor.transpose(state_ps[:, 1, :], cell_of[bt, "tanh"][GATE_O][:, jc, :], ident_f32[:])
+            cell_of[n, "state_ps"] = state_ps
+
+        def kept_and_fresh(n, step):
+            bt, jc = divmod(n, N_JC)
+            tanh = cell_of[bt, "tanh"]
+            kept = cell_pool.tile([P, P], F32)
             nc.vector.scalar_tensor_tensor(
                 out=kept[:],
-                in0=tanh_gate[:, :, GATE_F, :],
+                in0=tanh[GATE_F][:, jc, :],
                 scalar=1.0,
-                in1=cell_of[bt, "c_t_ps"][:],
+                in1=c_t_ps(step - 1),
                 op0=ALU.add,
                 op1=ALU.mult,
             )
-            fresh = cell_pool.tile([P, N_JC, P], F32)
+            fresh = cell_pool.tile([P, P], F32)
             nc.vector.scalar_tensor_tensor(
                 out=fresh[:],
-                in0=tanh_gate[:, :, GATE_I, :],
+                in0=tanh[GATE_I][:, jc, :],
                 scalar=1.0,
-                in1=cell_of[bt, "tanh_g_ps"][:],
+                in1=tanh_g_ps(step - 1),
                 op0=ALU.add,
                 op1=ALU.mult,
             )
-            cell_of[bt, "kept"] = kept
-            cell_of[bt, "fresh"] = fresh
+            terms_of[n] = (kept, fresh)
 
-        def new_state(bt):
-            b_rows = slice(bt * P, (bt + 1) * P)
-            c_twice_ps = psum_move.tile([P, H], F32, tag="move")
-            for jc in range(N_JC):
-                for i, term in enumerate((cell_of[bt, "kept"], cell_of[bt, "fresh"])):
-                    nc.tensor.matmul(
-                        out=c_twice_ps[:, jc * P : (jc + 1) * P],
-                        lhsT=term[:, jc, :],
-                        rhs=ident_f32[:],
-                        is_transpose=True,
-                        start=(i == 0),
-                        stop=(i == 1),
-                    )
-            c_new = out_pool.tile([P, H], F32)
-            nc.scalar.mul(out=c_new[:], in_=c_twice_ps[:], mul=0.5)
-            nc.sync.dma_start(out=out_1[b_rows, :], in_=c_new[:])
-            tanh_c = cell_pool.tile([P, H], F32)
-            nc.scalar.activation(out=tanh_c[:], in_=c_twice_ps[:], func=FUNC.Tanh, scale=0.5)
-            o_twice_ps = psum_move.tile([P, H], F32, tag="move")
-            for jc in range(N_JC):
-                nc.tensor.transpose(
-                    o_twice_ps[:, jc * P : (jc + 1) * P], cell_of[bt, "tanh_gate"][:, jc, GATE_O, :], ident_f32[:]
-                )
-            cell_of[bt, "tanh_c"] = tanh_c
-            cell_of[bt, "o_twice_ps"] = o_twice_ps
+        def new_state(n):
+            bt, jc = divmod(n, N_JC)
+            if jc == 0:
+                c_new = out_pool.tile([P, H], F32)
+                h_new = out_pool.tile([P, H], F32)
+                cell_of[bt, "out"] = (c_new, h_new)
+            c_new = cell_of[bt, "out"][0]
+            c_twice_ps = cell_of[n, "state_ps"][:, 0, :]
+            tanh_c = cell_pool.tile([P, P], F32)
+            nc.scalar.activation(out=tanh_c[:], in_=c_twice_ps, func=FUNC.Tanh, scale=0.5)
+            nc.scalar.mul(out=c_new[:, jc * P : (jc + 1) * P], in_=c_twice_ps, mul=0.5)
+            cell_of[n, "tanh_c"] = tanh_c
+            if jc == N_JC - 1:
+                nc.sync.dma_start(out=out_1[bt * P : (bt + 1) * P, :], in_=c_new[:])
 
-        def new_output(bt):
-            h_new = out_pool.tile([P, H], F32)
+        def new_output(n):
+            bt, jc = divmod(n, N_JC)
+            h_new = cell_of[bt, "out"][1]
             nc.vector.scalar_tensor_tensor(
-                out=h_new[:],
-                in0=cell_of[bt, "o_twice_ps"][:],
+                out=h_new[:, jc * P : (jc + 1) * P],
+                in0=cell_of[n, "state_ps"][:, 1, :],
                 scalar=0.5,
-                in1=cell_of[bt, "tanh_c"][:],
+                in1=cell_of[n, "tanh_c"][:],
                 op0=ALU.mult,
                 op1=ALU.mult,
             )
-            nc.sync.dma_start(out=out_0[bt * P : (bt + 1) * P, :], in_=h_new[:])
+            if jc == N_JC - 1:
+                nc.sync.dma_start(out=out_0[bt * P : (bt + 1) * P, :], in_=h_new[:])
 
         first_half = slice(0, H)
         second_half = slice(H, 2 * H)
@@ -386,12 +434,10 @@ def tile_decoderlstm_pa_t_kernel(
                 (W_hh0, first_half, w_h_q, first_chunk, 4),
                 (W_ih0, second_half, w_att_q, first_chunk, 4),
             ]
+        later_raw = []
         later_grouped = []
 
-        first_gate_step = len(later) + 1
-
-        def gate_step(n):
-            return max(n + 8, first_gate_step + n // 2)
+        transposed_in = [-1] * 2 + [0] * 2 + [1] * 2 + [2] * 2 + [3] * 2 + [4] * 2 + [5] * 2 + [6]
 
         def for_chunk(c, *stages):
             if 0 <= c < N_CHUNKS:
@@ -404,42 +450,61 @@ def tile_decoderlstm_pa_t_kernel(
                 for stage in stages:
                     stage(bt)
 
-        def for_gated_tile(step, *stages):
-            for bt in range(N_BT):
-                if gate_step(bt * N_JC + N_JC - 1) == step:
-                    for stage in stages:
-                        stage(bt)
+        def multiply_and_sum(step, run, multiplied, gates_to_do):
+            job = step - 9
+            if is_chunk(step - 2):
+                if gates_to_do:
+                    target = gates_of[job][:, gates_to_do[-1], :]
+                    while multiplied + is_chunk(job) * 3 * PASS_COLUMNS * len(gates_to_do) < QUOTA[run]:
+                        idle_pass(target)
+                        multiplied += PASS_COLUMNS
+            if is_chunk(job):
+                for gate in gates_to_do:
+                    gate_product(job, gate)
+            for_chunk(step - 2, lambda c: sum_over_s(c, run))
+
+        def is_chunk(c):
+            return 0 <= c < N_CHUNKS
+
+        def of_later(step, stage):
+            for n in range(len(later)):
+                if transposed_in[n] == step:
+                    stage(n)
 
         with tc.manual_schedule():
-            for group in first:
-                quantise(group, bring_k_to_partitions(group))
+            first_raw = [load_rows(group) for group in first]
+            for group, raw in zip(first, first_raw):
+                quantise(group, bring_k_to_partitions(raw, group[-1]))
 
-            for step in range(-4, N_CHUNKS + 10):
-                for_gated_tile(step - 1, kept_and_fresh)
-                for_gated_tile(step - 2, new_output)
+            for step in range(-4, N_CHUNKS + 13):
+                job = step - 9
+                if is_chunk(job) or is_chunk(step - 2):
+                    open_gates(job)
+                if is_chunk(job) and job % N_JC == 0:
+                    load_c(job // N_JC)
                 for_tile(step - 6, one_over_e_sum)
                 for_chunk(step, max_into_psum)
+                of_later(step, lambda n: later_grouped.append(bring_k_to_partitions(later_raw[n], later[n][-1])))
+                multiply_and_sum(step, 0, 4 * PASS_COLUMNS, (0, 1))
+                for_tile(step - 7, attention_rows)
                 for_chunk(step + 1, scores)
+                for_chunk(step - 12, new_output)
                 for_chunk(step, subtract_max)
-                for_tile(step - 6, attention)
+                for_chunk(step - 11, lambda n: kept_and_fresh(n, step))
+                for_tile(step - 8, quantise_attention)
                 for_chunk(step + 1, max_over_s)
                 for_chunk(step, exponential)
-                for_chunk(step - 2, sum_over_s)
+                multiply_and_sum(step, 1, 0, (2, 3))
                 for_chunk(step + 2, lin_into_psum)
-                for_tile(step - 7, group_attention, quantise_attention)
-                if 0 <= step - 1 < len(later):
-                    quantise(later[step - 1], later_grouped[step - 1])
+                for_chunk(step - 10, lambda n: cell_inputs(n, step))
+                multiply_and_sum(step, 2, 0, ())
+                for_chunk(step - 10, lambda n: transpose_c(n, step))
+                for_chunk(step - 11, transpose_state, new_state)
+                for_tile(step - 7, group_attention)
+                for_tile(step - 6, attention)
+                of_later(step - 1, lambda n: quantise(later[n], later_grouped[n]))
                 for_chunk(step - 1, weigh_enc)
-                for n in range(N_CHUNKS):
-                    bt, jc = divmod(n, N_JC)
-                    if gate_step(n) == step:
-                        if jc == 0:
-                            load_c(bt)
-                        gates(bt, jc)
-                if 0 <= step < len(later):
-                    later_grouped.append(bring_k_to_partitions(later[step]))
-                for_tile(step - 6, attention_rows)
+                for_chunk(job, tanh_of_gates)
+                of_later(step + 2, lambda n: later_raw.append(load_rows(later[n])))
                 for_tile(step - 5, log_of_e_sum)
                 for_tile(step + 4, load_enc, attn_lin)
-                for_gated_tile(step - 1, new_state)
-                for_gated_tile(step, cell_inputs)

@@ -15,22 +15,27 @@ INNER_TWO = mybir.AxisListType.XY
 
 P = 128
 PACK = 4
+PART = 4
 K_PASS = P * PACK
 PAIRS = K_PASS // 2
 B, H, S = 1024, 512, 16
 N_BT = B // P
 N_JC = H // P
 N_CHUNKS = N_BT * N_JC
+LAST = N_CHUNKS - 1
+MULTIPLIED = (8,)
+SBUF_JOBS = N_CHUNKS - 8
 N_GATES = 4
 GATE_I, GATE_F, GATE_G, GATE_O = 0, 1, 2, 3
 N_GC = N_GATES * N_JC
 S_RUN = 2
 S_OUT = S // S_RUN
-S_OUT_VECTOR = 4
+S_OUT_VECTOR = 5
 JC_PER_BANK = N_JC // 2
-N_RUNS = 3
+N_RUNS = 2
 RUN = -(-2 * S // N_RUNS)
-QUOTA = (2048, 1024, 0)
+QUOTA = (1280, 1152, 1024)
+EARLY_QUOTA = (2560, 1280, 1280)
 PASS_COLUMNS = 128
 GATE_SCALE = (0.5, 0.5, 1.0, 0.5)
 
@@ -44,7 +49,7 @@ def tile_decoderlstm_pa_t_kernel(
     with ExitStack() as ctx:
         keep = ctx.enter_context(tc.tile_pool(name="keep", bufs=1))
         raw_pool = ctx.enter_context(tc.tile_pool(name="raw", bufs=4))
-        grouped_pool = ctx.enter_context(tc.tile_pool(name="grouped", bufs=3))
+        grouped_pool = ctx.enter_context(tc.tile_pool(name="grouped", bufs=2))
         enc_pool = ctx.enter_context(tc.tile_pool(name="enc", bufs=2))
         scores_pool = ctx.enter_context(tc.tile_pool(name="scores", bufs=3))
         top_pool = ctx.enter_context(tc.tile_pool(name="top", bufs=3))
@@ -69,11 +74,11 @@ def tile_decoderlstm_pa_t_kernel(
         def row_ps(c):
             return both_rows_ps[c % 2][:, 0, :]
 
-        def tanh_g_ps(step):
-            return both_rows_ps[step % 2][:, 1, :]
+        def tanh_g_ps(n):
+            return both_rows_ps[n % 2][:, 1, :]
 
-        def c_t_ps(step):
-            return both_rows_ps[step % 2][:, 2, :].bitcast(BF16)[:, 0:P]
+        def c_t_ps(n):
+            return both_rows_ps[n % 2][:, 2, :].bitcast(BF16)[:, 0:P]
 
         bias_rows = keep.tile([P, P], BF16)
         nc.vector.memset(bias_rows[:].bitcast(I32), 0)
@@ -107,37 +112,42 @@ def tile_decoderlstm_pa_t_kernel(
         w_att_q = operand_tiles(N_GC, "w_att")
         w_h_q = operand_tiles(N_GC, "w_h")
 
-        def load_rows(group):
-            matrix, k_cols, operand, first_chunk, n_chunks = group
-            rows = matrix[first_chunk * P : (first_chunk + n_chunks) * P, k_cols]
-            raw = raw_pool.tile([P, n_chunks, K_PASS], BF16)
-            nc.sync.dma_start(out=raw[:], in_=rows.rearrange("(a r) k -> r a k", r=P))
+        grouped_of = {}
+
+        def load_rows(group, part):
+            name, matrix, k_cols, operand, first_chunk, n_chunks = group
+            first_row = (first_chunk + part * PART) * P
+            raw = raw_pool.tile([P, PART, K_PASS], BF16)
+            nc.sync.dma_start(
+                out=raw[:], in_=matrix[first_row : first_row + PART * P, k_cols].rearrange("(a r) k -> r a k", r=P)
+            )
             return raw
 
-        def bring_k_to_partitions(raw, n_chunks):
+        def bring_k_to_partitions(group, part, raw, copy):
+            if part == 0:
+                grouped = grouped_pool.tile([P, group[-1], P, PACK], BF16, align_bytes=64)
+                grouped_of[group[0]] = grouped
             raw_pairs = raw[:].bitcast(F32)
-            grouped = grouped_pool.tile([P, n_chunks, P, PACK], BF16, align_bytes=64)
-            grouped_pairs = grouped[:].bitcast(F32)
-            for a0 in range(0, n_chunks, 2):
+            grouped_pairs = grouped_of[group[0]][:, part * PART : (part + 1) * PART, :, :].bitcast(F32)
+            for a0 in range(0, PART, 2):
                 k_first = psum_move.tile([P, 2, 2, P], F32, tag="move")
                 for a in range(2):
                     for u in range(2):
                         nc.tensor.transpose(k_first[:, a, u, :], raw_pairs[:, a0 + a, u:PAIRS:2], ident_f32[:])
-                nc.scalar.copy(out=grouped_pairs[:, a0 : a0 + 2, :, :], in_=k_first[:].rearrange("p a u r -> p a r u"))
-            return grouped
+                copy(out=grouped_pairs[:, a0 : a0 + 2, :, :], in_=k_first[:].rearrange("p a u r -> p a r u"))
 
-        def quantise(group, grouped):
-            matrix, k_cols, operand, first_chunk, n_chunks = group
+        def quantise(group):
+            name, matrix, k_cols, operand, first_chunk, n_chunks = group
             words, scales = operand
             chunks = slice(first_chunk, first_chunk + n_chunks)
             nc.vector.quantize_mx(
                 out=words[:, chunks, :].rearrange("p a r -> p (a r)").bitcast(FP8X4),
                 scales=scales[:, chunks, :].rearrange("p a r -> p (a r)"),
-                in_=grouped[:].rearrange("p a r t -> p (a r t)"),
+                in_=grouped_of[group[0]][:].rearrange("p a r t -> p (a r t)"),
             )
 
         enc_of, lin_t_of, scores_of, top_of, e_of, enc_e_of = {}, {}, {}, {}, {}, {}
-        sums_of, gates_of, cell_of, terms_of = {}, {}, {}, {}
+        bank_of, sums_of, gates_of, cell_of, terms_of = {}, {}, {}, {}, {}
 
         def load_enc(bt):
             enc_sb = enc_pool.tile([P, S, H], BF16)
@@ -217,7 +227,8 @@ def tile_decoderlstm_pa_t_kernel(
         def weigh_enc(c):
             bt, jc = divmod(c, N_JC)
             enc_e = prod_pool.tile([P, S, P], F32)
-            nc.gpsimd.tensor_tensor(
+            engine = nc.vector if c == LAST else nc.gpsimd
+            engine.tensor_tensor(
                 out=enc_e[:], in0=enc_of[bt][:, :, jc * P : (jc + 1) * P], in1=e_of[c][:], op=ALU.mult
             )
             enc_e_of[c] = enc_e
@@ -234,51 +245,73 @@ def tile_decoderlstm_pa_t_kernel(
             )
 
         def sum_over_s(c, run):
-            if c % JC_PER_BANK == 0 and run == 0:
-                sums_ps = psum_sums.tile([P, 2, JC_PER_BANK, P], F32)
-                sums_of[c // JC_PER_BANK] = sums_ps
-            sums_ps = sums_of[c // JC_PER_BANK]
+            if run == 0:
+                if c == LAST:
+                    e_sum_ps = psum_sums.tile([P, P], F32, tag="sums")
+                    enc_e_sum_ps = psum_move.tile([P, P], F32, tag="move")
+                    sums_of[c] = (e_sum_ps[:], enc_e_sum_ps[:])
+                elif c % JC_PER_BANK == 0:
+                    sums_ps = psum_sums.tile([P, 2, JC_PER_BANK, P], F32, tag="sums")
+                    bank_of[c // JC_PER_BANK] = sums_ps
+                if c < LAST:
+                    place = c % JC_PER_BANK
+                    pair = bank_of[c // JC_PER_BANK]
+                    sums_of[c] = (pair[:, 0, place, :], pair[:, 1, place, :])
             terms = [(i, tile, s) for i, tile in enumerate((e_of[c], enc_e_of[c])) for s in range(S)]
             for i, tile, s in terms[run * RUN : (run + 1) * RUN]:
                 nc.tensor.matmul(
-                    out=sums_ps[:, i, c % JC_PER_BANK, :],
+                    out=sums_of[c][i],
                     lhsT=tile[:, s, :],
                     rhs=ident_f32[:],
-                    is_transpose=True,
+                    is_transpose=s not in MULTIPLIED,
                     start=(s == 0),
                     stop=(s == S - 1),
                 )
 
-        def chunks_of(half):
-            return slice(half * JC_PER_BANK, (half + 1) * JC_PER_BANK)
+        def bank(bt, k):
+            if bt == N_BT - 1 and k > 0:
+                jc = JC_PER_BANK + k - 1
+                e_sum, enc_e_sum = sums_of[bt * N_JC + jc]
+                return slice(jc, jc + 1), e_sum.unsqueeze(1), enc_e_sum.unsqueeze(1)
+            pair = bank_of[2 * bt + k]
+            return slice(k * JC_PER_BANK, (k + 1) * JC_PER_BANK), pair[:, 0, :, :], pair[:, 1, :, :]
+
+        def by_scalar(bt):
+            return 1 if bt == N_BT - 1 else 2
 
         def log_of_e_sum(bt):
             inv_t = row_pool.tile([P, N_JC, P], F32)
-            for half in range(2):
-                nc.scalar.activation(out=inv_t[:, chunks_of(half), :], in_=sums_of[2 * bt + half][:, 0, :, :], func=FUNC.Ln)
+            for k in range(by_scalar(bt)):
+                jc, e_sum, enc_e_sum = bank(bt, k)
+                nc.scalar.activation(out=inv_t[:, jc, :], in_=e_sum, func=FUNC.Ln)
             cell_of[bt, "inv_t"] = inv_t
 
         def one_over_e_sum(bt):
-            inv_t = cell_of[bt, "inv_t"]
-            nc.scalar.activation(out=inv_t[:], in_=inv_t[:], func=FUNC.Exp, scale=-1.0)
+            inv_t = cell_of[bt, "inv_t"][:, 0 : by_scalar(bt) * JC_PER_BANK, :]
+            nc.scalar.activation(out=inv_t, in_=inv_t, func=FUNC.Exp, scale=-1.0)
+
+        def reciprocal_of_e_sum(bt, k):
+            jc, e_sum, enc_e_sum = bank(bt, k)
+            nc.vector.reciprocal(out=cell_of[bt, "inv_t"][:, jc, :], in_=e_sum)
 
         def attention(bt):
             att_t = row_pool.tile([P, N_JC, P], BF16)
-            for half in range(2):
+            for k in range(3 if bt == N_BT - 1 else 2):
+                jc, e_sum, enc_e_sum = bank(bt, k)
                 nc.vector.tensor_tensor(
-                    out=att_t[:, chunks_of(half), :],
-                    in0=sums_of[2 * bt + half][:, 1, :, :],
-                    in1=cell_of[bt, "inv_t"][:, chunks_of(half), :],
-                    op=ALU.mult,
+                    out=att_t[:, jc, :], in0=enc_e_sum, in1=cell_of[bt, "inv_t"][:, jc, :], op=ALU.mult
                 )
             cell_of[bt, "att_t"] = att_t
+
+        def copy_for(bt):
+            return nc.vector.tensor_copy if bt == N_BT - 1 else nc.scalar.copy
 
         def attention_rows(bt):
             att_ps = psum_move.tile([P, H], BF16, tag="move")
             for jc in range(N_JC):
                 nc.tensor.transpose(att_ps[:, jc * P : (jc + 1) * P], cell_of[bt, "att_t"][:, jc, :], ident_bf[:])
             att = row_pool.tile([P, H], BF16)
-            nc.scalar.copy(out=att[:], in_=att_ps[:])
+            copy_for(bt)(out=att[:], in_=att_ps[:])
             cell_of[bt, "att"] = att
 
         def group_attention(bt):
@@ -286,7 +319,7 @@ def tile_decoderlstm_pa_t_kernel(
             for t in range(PACK):
                 nc.tensor.transpose(att_k_ps[:, t, :], cell_of[bt, "att"][:, t:H:PACK], ident_bf[:])
             att_grouped = row_pool.tile([P, P, PACK], BF16, align_bytes=64)
-            nc.scalar.copy(out=att_grouped[:], in_=att_k_ps[:].rearrange("p t b -> p b t"))
+            copy_for(bt)(out=att_grouped[:], in_=att_k_ps[:].rearrange("p t b -> p b t"))
             cell_of[bt, "att_grouped"] = att_grouped
 
         def load_c(bt):
@@ -343,33 +376,49 @@ def tile_decoderlstm_pa_t_kernel(
                     scale=GATE_SCALE[gate],
                 )
             tanh_o = cell_of[bt, "tanh"][GATE_O][:, jc, :]
-            nc.scalar.add(out=tanh_o, in_=tanh_o, add=1.0)
+            if bt == N_BT - 1:
+                nc.vector.tensor_scalar_add(out=tanh_o, in0=tanh_o, scalar1=1.0)
+            else:
+                nc.scalar.add(out=tanh_o, in_=tanh_o, add=1.0)
 
-        def cell_inputs(n, step):
+        def cell_inputs(n):
             bt, jc = divmod(n, N_JC)
+            if n >= SBUF_JOBS:
+                return
             nc.tensor.matmul(
-                out=tanh_g_ps(step),
+                out=tanh_g_ps(n),
                 lhsT=ident_f32[:],
                 rhs=cell_of[bt, "tanh"][GATE_G][:, jc, :],
                 start=True,
                 stop=True,
             )
 
-        def transpose_c(n, step):
+        def transpose_c(n):
             bt, jc = divmod(n, N_JC)
-            nc.tensor.transpose(c_t_ps(step), cell_of[bt, "c_raw"][:, jc * P : (jc + 1) * P], ident_bf[:])
+            nc.tensor.transpose(c_t_ps(n), cell_of[bt, "c_raw"][:, jc * P : (jc + 1) * P], ident_bf[:])
 
-        def transpose_state(n):
-            bt, jc = divmod(n, N_JC)
-            state_ps = psum_move.tile([P, 2, P], F32, tag="move")
-            for i, term in enumerate(terms_of[n]):
-                nc.tensor.matmul(
-                    out=state_ps[:, 0, :], lhsT=term[:], rhs=ident_f32[:], is_transpose=True, start=(i == 0), stop=(i == 1)
-                )
-            nc.tensor.transpose(state_ps[:, 1, :], cell_of[bt, "tanh"][GATE_O][:, jc, :], ident_f32[:])
-            cell_of[n, "state_ps"] = state_ps
+        def transpose_states(jobs):
+            if not jobs:
+                return
+            if jobs[0] < SBUF_JOBS:
+                states_ps = psum_move.tile([P, 2, 2, P], F32, tag="move")
+            else:
+                states_ps = psum_sums.tile([P, 2, 2, P], F32, tag="sums")
+            for place, n in enumerate(jobs):
+                bt, jc = divmod(n, N_JC)
+                for i, term in enumerate(terms_of[n]):
+                    nc.tensor.matmul(
+                        out=states_ps[:, place, 0, :],
+                        lhsT=term[:],
+                        rhs=ident_f32[:],
+                        is_transpose=True,
+                        start=(i == 0),
+                        stop=(i == 1),
+                    )
+                nc.tensor.transpose(states_ps[:, place, 1, :], cell_of[bt, "tanh"][GATE_O][:, jc, :], ident_f32[:])
+                cell_of[n, "state_ps"] = states_ps[:, place, :, :]
 
-        def kept_and_fresh(n, step):
+        def kept_and_fresh(n):
             bt, jc = divmod(n, N_JC)
             tanh = cell_of[bt, "tanh"]
             kept = cell_pool.tile([P, P], F32)
@@ -377,7 +426,7 @@ def tile_decoderlstm_pa_t_kernel(
                 out=kept[:],
                 in0=tanh[GATE_F][:, jc, :],
                 scalar=1.0,
-                in1=c_t_ps(step - 1),
+                in1=c_t_ps(n),
                 op0=ALU.add,
                 op1=ALU.mult,
             )
@@ -386,7 +435,7 @@ def tile_decoderlstm_pa_t_kernel(
                 out=fresh[:],
                 in0=tanh[GATE_I][:, jc, :],
                 scalar=1.0,
-                in1=tanh_g_ps(step - 1),
+                in1=tanh[GATE_G][:, jc, :] if n >= SBUF_JOBS else tanh_g_ps(n),
                 op0=ALU.add,
                 op1=ALU.mult,
             )
@@ -402,7 +451,10 @@ def tile_decoderlstm_pa_t_kernel(
             c_twice_ps = cell_of[n, "state_ps"][:, 0, :]
             tanh_c = cell_pool.tile([P, P], F32)
             nc.scalar.activation(out=tanh_c[:], in_=c_twice_ps, func=FUNC.Tanh, scale=0.5)
-            nc.scalar.mul(out=c_new[:, jc * P : (jc + 1) * P], in_=c_twice_ps, mul=0.5)
+            if bt == N_BT - 1:
+                nc.vector.tensor_scalar_mul(out=c_new[:, jc * P : (jc + 1) * P], in0=c_twice_ps, scalar1=0.5)
+            else:
+                nc.scalar.mul(out=c_new[:, jc * P : (jc + 1) * P], in_=c_twice_ps, mul=0.5)
             cell_of[n, "tanh_c"] = tanh_c
             if jc == N_JC - 1:
                 nc.sync.dma_start(out=out_1[bt * P : (bt + 1) * P, :], in_=c_new[:])
@@ -424,20 +476,24 @@ def tile_decoderlstm_pa_t_kernel(
         first_half = slice(0, H)
         second_half = slice(H, 2 * H)
         half_batch = N_BT // 2
-        first = [(x, first_half, x_q, 0, half_batch), (attn_W, first_half, attn_w_q, 0, N_JC)]
-        later = [(x, first_half, x_q, half_batch, half_batch)]
-        for first_chunk in range(0, N_BT, 4):
-            later.append((h_prev, first_half, h_q, first_chunk, 4))
-        for first_chunk in range(0, N_GC, 4):
+        first = [("x0", x, first_half, x_q, 0, half_batch), ("attn_w", attn_W, first_half, attn_w_q, 0, N_JC)]
+        later = [("x1", x, first_half, x_q, half_batch, half_batch), ("h", h_prev, first_half, h_q, 0, N_BT)]
+        for half, first_chunk in (("0", 0), ("1", 8)):
             later += [
-                (W_ih0, first_half, w_x_q, first_chunk, 4),
-                (W_hh0, first_half, w_h_q, first_chunk, 4),
-                (W_ih0, second_half, w_att_q, first_chunk, 4),
+                ("w_x" + half, W_ih0, first_half, w_x_q, first_chunk, 8),
+                ("w_h" + half, W_hh0, first_half, w_h_q, first_chunk, 8),
+                ("w_att" + half, W_ih0, second_half, w_att_q, first_chunk, 8),
             ]
-        later_raw = []
-        later_grouped = []
+        parts = [(group, part) for group in later for part in range(group[-1] // PART)]
+        raw_of = {}
 
-        transposed_in = [-1] * 2 + [0] * 2 + [1] * 2 + [2] * 2 + [3] * 2 + [4] * 2 + [5] * 2 + [6]
+        transposed_in = [-1, -1, 0, 0, 1, 1, 2, 2, 3, 3, 4, 4, 5, 5, 6]
+        jobs_of = {}
+        for n in range(N_CHUNKS):
+            jobs_of.setdefault(max(n + 9, transposed_in[-1] + 2 + n // 2), []).append(n)
+
+        def jobs_in(step):
+            return jobs_of.get(step, [])
 
         def for_chunk(c, *stages):
             if 0 <= c < N_CHUNKS:
@@ -450,61 +506,121 @@ def tile_decoderlstm_pa_t_kernel(
                 for stage in stages:
                     stage(bt)
 
-        def multiply_and_sum(step, run, multiplied, gates_to_do):
-            job = step - 9
-            if is_chunk(step - 2):
-                if gates_to_do:
-                    target = gates_of[job][:, gates_to_do[-1], :]
-                    while multiplied + is_chunk(job) * 3 * PASS_COLUMNS * len(gates_to_do) < QUOTA[run]:
-                        idle_pass(target)
-                        multiplied += PASS_COLUMNS
-            if is_chunk(job):
+        def keep_multiplying(step, block, columns, target):
+            if is_chunk(step - 2) and is_chunk(step):
+                while columns < (QUOTA if jobs_in(step) else EARLY_QUOTA)[block]:
+                    idle_pass(target)
+                    columns += PASS_COLUMNS
+
+        def multiply_and_sum(step, run, columns, gates_to_do):
+            jobs = jobs_in(step)
+            columns += 3 * PASS_COLUMNS * len(gates_to_do) * len(jobs)
+            if jobs or is_chunk(step - 2):
+                keep_multiplying(step, run, columns, gates_of[jobs[-1] if jobs else None][:, gates_to_do[-1], :])
+            for n in jobs:
                 for gate in gates_to_do:
-                    gate_product(job, gate)
+                    gate_product(n, gate)
             for_chunk(step - 2, lambda c: sum_over_s(c, run))
 
         def is_chunk(c):
             return 0 <= c < N_CHUNKS
 
-        def of_later(step, stage):
-            for n in range(len(later)):
-                if transposed_in[n] == step:
-                    stage(n)
+        def for_parts(step, stage):
+            for part, when in zip(parts, transposed_in):
+                if when == step:
+                    stage(*part)
+
+        def load_part(group, part):
+            raw_of[group[0], part] = load_rows(group, part)
+
+        def transpose_part(group, part):
+            bring_k_to_partitions(group, part, raw_of[group[0], part], nc.scalar.copy)
+
+        def quantise_if_last(group, part):
+            if part == group[-1] // PART - 1:
+                quantise(group)
 
         with tc.manual_schedule():
-            first_raw = [load_rows(group) for group in first]
-            for group, raw in zip(first, first_raw):
-                quantise(group, bring_k_to_partitions(raw, group[-1]))
+            first_raw = [load_rows(group, 0) for group in first]
+            for group, raw, copy in zip(first, first_raw, (nc.scalar.copy, nc.vector.tensor_copy)):
+                bring_k_to_partitions(group, 0, raw, copy)
+            for group in first:
+                quantise(group)
 
-            for step in range(-4, N_CHUNKS + 13):
-                job = step - 9
-                if is_chunk(job) or is_chunk(step - 2):
-                    open_gates(job)
-                if is_chunk(job) and job % N_JC == 0:
-                    load_c(job // N_JC)
+            def for_jobs(step, *stages):
+                for n in jobs_in(step):
+                    for stage in stages:
+                        stage(n)
+
+            for step in range(-4, N_CHUNKS):
+                if not jobs_in(step) and is_chunk(step - 2):
+                    open_gates(None)
+                for n in jobs_in(step):
+                    open_gates(n)
+                    if n % N_JC == 0:
+                        load_c(n // N_JC)
                 for_tile(step - 6, one_over_e_sum)
                 for_chunk(step, max_into_psum)
-                of_later(step, lambda n: later_grouped.append(bring_k_to_partitions(later_raw[n], later[n][-1])))
+                for_parts(step, transpose_part)
                 multiply_and_sum(step, 0, 4 * PASS_COLUMNS, (0, 1))
                 for_tile(step - 7, attention_rows)
                 for_chunk(step + 1, scores)
-                for_chunk(step - 12, new_output)
+                for_jobs(step - 3, new_output)
                 for_chunk(step, subtract_max)
-                for_chunk(step - 11, lambda n: kept_and_fresh(n, step))
-                for_tile(step - 8, quantise_attention)
+                for_jobs(step - 2, kept_and_fresh)
                 for_chunk(step + 1, max_over_s)
+                for_tile(step - 8, quantise_attention)
+                for_parts(step, quantise_if_last)
                 for_chunk(step, exponential)
                 multiply_and_sum(step, 1, 0, (2, 3))
+                keep_multiplying(step, 2, 4 * PASS_COLUMNS * (1 + len(jobs_in(step - 1))), row_ps(step + 2))
                 for_chunk(step + 2, lin_into_psum)
-                for_chunk(step - 10, lambda n: cell_inputs(n, step))
-                multiply_and_sum(step, 2, 0, ())
-                for_chunk(step - 10, lambda n: transpose_c(n, step))
-                for_chunk(step - 11, transpose_state, new_state)
+                for_jobs(step - 1, cell_inputs, transpose_c)
+                transpose_states(jobs_in(step - 2))
+                for_jobs(step - 2, new_state)
                 for_tile(step - 7, group_attention)
                 for_tile(step - 6, attention)
-                of_later(step - 1, lambda n: quantise(later[n], later_grouped[n]))
                 for_chunk(step - 1, weigh_enc)
-                for_chunk(job, tanh_of_gates)
-                of_later(step + 2, lambda n: later_raw.append(load_rows(later[n])))
+                for_jobs(step, tanh_of_gates)
+                for_parts(step + 2, load_part)
                 for_tile(step - 5, log_of_e_sum)
                 for_tile(step + 4, load_enc, attn_lin)
+
+            last_bt = N_BT - 1
+            first_job = N_CHUNKS - 9
+
+            def start_job(n):
+                if is_chunk(n):
+                    if n % N_JC == 0:
+                        load_c(n // N_JC)
+                    open_gates(n)
+                    for gate in range(N_GATES):
+                        gate_product(n, gate)
+
+            def finish_jobs(n):
+                if n > first_job:
+                    for_chunk(n - 3, lambda m: transpose_states([m]), new_state)
+                for_chunk(n - 3 if n == first_job else n - 4, new_output)
+                for_chunk(n - 1, cell_inputs, transpose_c)
+                for_chunk(n - 2, kept_and_fresh)
+                for_chunk(n, tanh_of_gates)
+
+            weigh_enc(LAST)
+            quantise_attention(last_bt - 1)
+            start_job(first_job)
+            for run in range(N_RUNS):
+                sum_over_s(LAST - 1, run)
+            finish_jobs(first_job)
+            log_of_e_sum(last_bt)
+            one_over_e_sum(last_bt)
+            reciprocal_of_e_sum(last_bt, 1)
+            for run in range(N_RUNS):
+                sum_over_s(LAST, run)
+            reciprocal_of_e_sum(last_bt, 2)
+            attention(last_bt)
+            attention_rows(last_bt)
+            group_attention(last_bt)
+            quantise_attention(last_bt)
+            for n in range(first_job + 1, N_CHUNKS + 4):
+                start_job(n)
+                finish_jobs(n)

@@ -23,8 +23,8 @@ N_BT = B // P
 N_JC = H // P
 N_CHUNKS = N_BT * N_JC
 LAST = N_CHUNKS - 1
-MULTIPLIED = (8,)
 SBUF_JOBS = N_CHUNKS - 8
+FREE_BANK_JOB = N_CHUNKS - 7
 N_GATES = 4
 GATE_I, GATE_F, GATE_G, GATE_O = 0, 1, 2, 3
 N_GC = N_GATES * N_JC
@@ -34,8 +34,8 @@ S_OUT_VECTOR = 5
 JC_PER_BANK = N_JC // 2
 N_RUNS = 2
 RUN = -(-2 * S // N_RUNS)
-QUOTA = (1280, 1152, 1024)
-EARLY_QUOTA = (2560, 1280, 1280)
+QUOTA = (1280, 1280, 1280)
+EARLY_QUOTA = (2560, 1408, 1408)
 PASS_COLUMNS = 128
 GATE_SCALE = (0.5, 0.5, 1.0, 0.5)
 
@@ -48,12 +48,13 @@ def tile_decoderlstm_pa_t_kernel(
     nc = tc.nc
     with ExitStack() as ctx:
         keep = ctx.enter_context(tc.tile_pool(name="keep", bufs=1))
-        raw_pool = ctx.enter_context(tc.tile_pool(name="raw", bufs=4))
+        raw_pool = ctx.enter_context(tc.tile_pool(name="raw", bufs=3))
+        pairs_pool = ctx.enter_context(tc.tile_pool(name="pairs", bufs=3))
         grouped_pool = ctx.enter_context(tc.tile_pool(name="grouped", bufs=2))
         enc_pool = ctx.enter_context(tc.tile_pool(name="enc", bufs=2))
         scores_pool = ctx.enter_context(tc.tile_pool(name="scores", bufs=3))
         top_pool = ctx.enter_context(tc.tile_pool(name="top", bufs=3))
-        e_pool = ctx.enter_context(tc.tile_pool(name="e", bufs=4))
+        e_pool = ctx.enter_context(tc.tile_pool(name="e", bufs=3))
         prod_pool = ctx.enter_context(tc.tile_pool(name="prod", bufs=3))
         row_pool = ctx.enter_context(tc.tile_pool(name="row", bufs=2))
         att_pool = ctx.enter_context(tc.tile_pool(name="att", bufs=4))
@@ -123,17 +124,21 @@ def tile_decoderlstm_pa_t_kernel(
             )
             return raw
 
+        def part_pairs(raw):
+            pairs = pairs_pool.tile([P, PART, 2, P], F32)
+            nc.scalar.copy(out=pairs[:], in_=raw[:].bitcast(F32).rearrange("p a (w u) -> p a u w", u=2))
+            return pairs
+
         def bring_k_to_partitions(group, part, raw, copy):
             if part == 0:
                 grouped = grouped_pool.tile([P, group[-1], P, PACK], BF16, align_bytes=64)
                 grouped_of[group[0]] = grouped
-            raw_pairs = raw[:].bitcast(F32)
             grouped_pairs = grouped_of[group[0]][:, part * PART : (part + 1) * PART, :, :].bitcast(F32)
             for a0 in range(0, PART, 2):
                 k_first = psum_move.tile([P, 2, 2, P], F32, tag="move")
                 for a in range(2):
                     for u in range(2):
-                        nc.tensor.transpose(k_first[:, a, u, :], raw_pairs[:, a0 + a, u:PAIRS:2], ident_f32[:])
+                        nc.tensor.transpose(k_first[:, a, u, :], raw[:, a0 + a, u, :], ident_f32[:])
                 copy(out=grouped_pairs[:, a0 : a0 + 2, :, :], in_=k_first[:].rearrange("p a u r -> p a r u"))
 
         def quantise(group):
@@ -187,7 +192,7 @@ def tile_decoderlstm_pa_t_kernel(
 
         def scores(c):
             bt, jc = divmod(c, N_JC)
-            sc = scores_pool.tile([P, S_OUT, P, S_RUN], F32)
+            sc = scores_pool.tile([P, S_OUT, P, S_RUN], F32, tag="scores")
             nc.vector.tensor_tensor(
                 out=sc[:],
                 in0=for_s(row_ps(c), S_OUT),
@@ -246,57 +251,48 @@ def tile_decoderlstm_pa_t_kernel(
 
         def sum_over_s(c, run):
             if run == 0:
-                if c == LAST:
-                    e_sum_ps = psum_sums.tile([P, P], F32, tag="sums")
-                    enc_e_sum_ps = psum_move.tile([P, P], F32, tag="move")
-                    sums_of[c] = (e_sum_ps[:], enc_e_sum_ps[:])
-                elif c % JC_PER_BANK == 0:
+                if c % JC_PER_BANK == 0:
                     sums_ps = psum_sums.tile([P, 2, JC_PER_BANK, P], F32, tag="sums")
                     bank_of[c // JC_PER_BANK] = sums_ps
-                if c < LAST:
-                    place = c % JC_PER_BANK
-                    pair = bank_of[c // JC_PER_BANK]
-                    sums_of[c] = (pair[:, 0, place, :], pair[:, 1, place, :])
+                place = c % JC_PER_BANK
+                pair = bank_of[c // JC_PER_BANK]
+                sums_of[c] = (pair[:, 0, place, :], pair[:, 1, place, :])
             terms = [(i, tile, s) for i, tile in enumerate((e_of[c], enc_e_of[c])) for s in range(S)]
             for i, tile, s in terms[run * RUN : (run + 1) * RUN]:
                 nc.tensor.matmul(
                     out=sums_of[c][i],
                     lhsT=tile[:, s, :],
                     rhs=ident_f32[:],
-                    is_transpose=s not in MULTIPLIED,
+                    is_transpose=True,
                     start=(s == 0),
                     stop=(s == S - 1),
                 )
 
+        last_sums = []
+
         def bank(bt, k):
             if bt == N_BT - 1 and k > 0:
-                jc = JC_PER_BANK + k - 1
-                e_sum, enc_e_sum = sums_of[bt * N_JC + jc]
-                return slice(jc, jc + 1), e_sum.unsqueeze(1), enc_e_sum.unsqueeze(1)
+                e_sum, enc_e_sum = sums_of[LAST - 1]
+                return slice(JC_PER_BANK, N_JC - 1), e_sum.unsqueeze(1), enc_e_sum.unsqueeze(1)
             pair = bank_of[2 * bt + k]
             return slice(k * JC_PER_BANK, (k + 1) * JC_PER_BANK), pair[:, 0, :, :], pair[:, 1, :, :]
 
-        def by_scalar(bt):
-            return 1 if bt == N_BT - 1 else 2
-
         def log_of_e_sum(bt):
             inv_t = row_pool.tile([P, N_JC, P], F32)
-            for k in range(by_scalar(bt)):
+            for k in range(2):
                 jc, e_sum, enc_e_sum = bank(bt, k)
                 nc.scalar.activation(out=inv_t[:, jc, :], in_=e_sum, func=FUNC.Ln)
+            if bt == N_BT - 1:
+                nc.scalar.activation(out=inv_t[:, N_JC - 1, :], in_=last_sums[0], func=FUNC.Ln)
             cell_of[bt, "inv_t"] = inv_t
 
         def one_over_e_sum(bt):
-            inv_t = cell_of[bt, "inv_t"][:, 0 : by_scalar(bt) * JC_PER_BANK, :]
-            nc.scalar.activation(out=inv_t, in_=inv_t, func=FUNC.Exp, scale=-1.0)
-
-        def reciprocal_of_e_sum(bt, k):
-            jc, e_sum, enc_e_sum = bank(bt, k)
-            nc.vector.reciprocal(out=cell_of[bt, "inv_t"][:, jc, :], in_=e_sum)
+            inv_t = cell_of[bt, "inv_t"]
+            nc.scalar.activation(out=inv_t[:], in_=inv_t[:], func=FUNC.Exp, scale=-1.0)
 
         def attention(bt):
             att_t = row_pool.tile([P, N_JC, P], BF16)
-            for k in range(3 if bt == N_BT - 1 else 2):
+            for k in range(2):
                 jc, e_sum, enc_e_sum = bank(bt, k)
                 nc.vector.tensor_tensor(
                     out=att_t[:, jc, :], in0=enc_e_sum, in1=cell_of[bt, "inv_t"][:, jc, :], op=ALU.mult
@@ -307,12 +303,34 @@ def tile_decoderlstm_pa_t_kernel(
             return nc.vector.tensor_copy if bt == N_BT - 1 else nc.scalar.copy
 
         def attention_rows(bt):
+            n_jc = N_JC - 1 if bt == N_BT - 1 else N_JC
             att_ps = psum_move.tile([P, H], BF16, tag="move")
-            for jc in range(N_JC):
+            for jc in range(n_jc):
                 nc.tensor.transpose(att_ps[:, jc * P : (jc + 1) * P], cell_of[bt, "att_t"][:, jc, :], ident_bf[:])
-            att = row_pool.tile([P, H], BF16)
-            copy_for(bt)(out=att[:], in_=att_ps[:])
-            cell_of[bt, "att"] = att
+            copy_for(bt)(out=att_tile(bt)[:, 0 : n_jc * P], in_=att_ps[:, 0 : n_jc * P])
+
+        def att_tile(bt):
+            if (bt, "att") not in cell_of:
+                att = row_pool.tile([P, H], BF16)
+                cell_of[bt, "att"] = att
+            return cell_of[bt, "att"]
+
+        def sum_by_vector(terms):
+            sums = scores_pool.tile([P, S // 2, P], F32, tag="scores")
+            n = S // 2
+            while n > 0:
+                nc.vector.tensor_tensor(out=sums[:, 0:n, :], in0=terms[:, 0:n, :], in1=terms[:, n : 2 * n, :], op=ALU.add)
+                terms = sums
+                n //= 2
+            return sums[:, 0, :]
+
+        def last_attention_by_vector():
+            nc.vector.tensor_tensor(
+                out=att_tile(N_BT - 1)[:, (N_JC - 1) * P : H],
+                in0=last_sums[1],
+                in1=cell_of[N_BT - 1, "inv_t"][:, N_JC - 1, :],
+                op=ALU.mult,
+            )
 
         def group_attention(bt):
             att_k_ps = psum_move.tile([P, PACK, P], BF16, tag="move")
@@ -338,7 +356,10 @@ def tile_decoderlstm_pa_t_kernel(
             cell_of[bt, "att_q"] = (att_words, att_scales)
 
         def open_gates(n):
-            gates_ps = psum_move.tile([P, N_GATES, P], F32, tag="move")
+            if n == FREE_BANK_JOB:
+                gates_ps = psum_sums.tile([P, N_GATES, P], F32, tag="sums")
+            else:
+                gates_ps = psum_move.tile([P, N_GATES, P], F32, tag="move")
             gates_of[n] = gates_ps
 
         def gate_product(n, gate):
@@ -536,12 +557,16 @@ def tile_decoderlstm_pa_t_kernel(
         def transpose_part(group, part):
             bring_k_to_partitions(group, part, raw_of[group[0], part], nc.scalar.copy)
 
+        def pair_part(group, part):
+            raw_of[group[0], part] = part_pairs(raw_of[group[0], part])
+
         def quantise_if_last(group, part):
             if part == group[-1] // PART - 1:
                 quantise(group)
 
         with tc.manual_schedule():
             first_raw = [load_rows(group, 0) for group in first]
+            first_raw = [part_pairs(raw) for raw in first_raw]
             for group, raw, copy in zip(first, first_raw, (nc.scalar.copy, nc.vector.tensor_copy)):
                 bring_k_to_partitions(group, 0, raw, copy)
             for group in first:
@@ -582,6 +607,7 @@ def tile_decoderlstm_pa_t_kernel(
                 for_tile(step - 6, attention)
                 for_chunk(step - 1, weigh_enc)
                 for_jobs(step, tanh_of_gates)
+                for_parts(step + 1, pair_part)
                 for_parts(step + 2, load_part)
                 for_tile(step - 5, log_of_e_sum)
                 for_tile(step + 4, load_enc, attn_lin)
@@ -589,12 +615,13 @@ def tile_decoderlstm_pa_t_kernel(
             last_bt = N_BT - 1
             first_job = N_CHUNKS - 9
 
-            def start_job(n):
+            def start_job(n, gates_to_do):
                 if is_chunk(n):
-                    if n % N_JC == 0:
-                        load_c(n // N_JC)
-                    open_gates(n)
-                    for gate in range(N_GATES):
+                    if gates_to_do[0] == 0:
+                        if n % N_JC == 0:
+                            load_c(n // N_JC)
+                        open_gates(n)
+                    for gate in gates_to_do:
                         gate_product(n, gate)
 
             def finish_jobs(n):
@@ -603,24 +630,30 @@ def tile_decoderlstm_pa_t_kernel(
                 for_chunk(n - 3 if n == first_job else n - 4, new_output)
                 for_chunk(n - 1, cell_inputs, transpose_c)
                 for_chunk(n - 2, kept_and_fresh)
-                for_chunk(n, tanh_of_gates)
 
-            weigh_enc(LAST)
+            last_sums.append(sum_by_vector(e_of[LAST]))
             quantise_attention(last_bt - 1)
-            start_job(first_job)
-            for run in range(N_RUNS):
-                sum_over_s(LAST - 1, run)
-            finish_jobs(first_job)
+            weigh_enc(LAST)
+            sum_over_s(LAST - 1, 0)
             log_of_e_sum(last_bt)
             one_over_e_sum(last_bt)
-            reciprocal_of_e_sum(last_bt, 1)
-            for run in range(N_RUNS):
-                sum_over_s(LAST, run)
-            reciprocal_of_e_sum(last_bt, 2)
+            start_job(first_job, range(N_GATES))
+            sum_over_s(LAST - 1, 1)
+            tanh_of_gates(first_job)
+            finish_jobs(first_job)
+            last_sums.append(sum_by_vector(enc_e_of[LAST]))
+            start_job(first_job + 1, range(N_GATES))
+            tanh_of_gates(first_job + 1)
             attention(last_bt)
+            last_attention_by_vector()
+            start_job(first_job + 2, range(N_GATES))
             attention_rows(last_bt)
             group_attention(last_bt)
             quantise_attention(last_bt)
-            for n in range(first_job + 1, N_CHUNKS + 4):
-                start_job(n)
+            finish_jobs(first_job + 1)
+            tanh_of_gates(first_job + 2)
+            finish_jobs(first_job + 2)
+            for n in range(first_job + 3, N_CHUNKS + 4):
+                start_job(n, range(N_GATES))
                 finish_jobs(n)
+                for_chunk(n, tanh_of_gates)

@@ -25,6 +25,7 @@ N_CHUNKS = N_BT * N_JC
 LAST = N_CHUNKS - 1
 SBUF_JOBS = N_CHUNKS - 8
 FREE_BANK_JOB = N_CHUNKS - 7
+FIRST_JOB_STEP = 9
 N_GATES = 4
 GATE_I, GATE_F, GATE_G, GATE_O = 0, 1, 2, 3
 N_GC = N_GATES * N_JC
@@ -32,11 +33,6 @@ S_RUN = 2
 S_OUT = S // S_RUN
 S_OUT_VECTOR = 5
 JC_PER_BANK = N_JC // 2
-N_RUNS = 2
-RUN = -(-2 * S // N_RUNS)
-QUOTA = (1280, 1280, 1280)
-EARLY_QUOTA = (2560, 1408, 1408)
-PASS_COLUMNS = 128
 GATE_SCALE = (0.5, 0.5, 1.0, 0.5)
 
 FLOPS = 2 * B * H * H + 2 * B * (3 * H) * (N_GATES * H)
@@ -76,10 +72,10 @@ def tile_decoderlstm_pa_t_kernel(
             return both_rows_ps[c % 2][:, 0, :]
 
         def tanh_g_ps(n):
-            return both_rows_ps[n % 2][:, 1, :]
+            return both_rows_ps[(n + 1) % 2][:, 1, :]
 
         def c_t_ps(n):
-            return both_rows_ps[n % 2][:, 2, :].bitcast(BF16)[:, 0:P]
+            return both_rows_ps[(n + 1) % 2][:, 2, :].bitcast(BF16)[:, 0:P]
 
         bias_rows = keep.tile([P, P], BF16)
         nc.vector.memset(bias_rows[:].bitcast(I32), 0)
@@ -152,7 +148,7 @@ def tile_decoderlstm_pa_t_kernel(
             )
 
         enc_of, lin_t_of, scores_of, top_of, e_of, enc_e_of = {}, {}, {}, {}, {}, {}
-        bank_of, sums_of, gates_of, cell_of, terms_of = {}, {}, {}, {}, {}
+        bank_of, gates_of, cell_of, terms_of = {}, {}, {}, {}
 
         def load_enc(bt):
             enc_sb = enc_pool.tile([P, S, H], BF16)
@@ -232,38 +228,23 @@ def tile_decoderlstm_pa_t_kernel(
         def weigh_enc(c):
             bt, jc = divmod(c, N_JC)
             enc_e = prod_pool.tile([P, S, P], F32)
-            engine = nc.vector if c == LAST else nc.gpsimd
+            engine = nc.vector if c >= LAST - 1 else nc.gpsimd
             engine.tensor_tensor(
                 out=enc_e[:], in0=enc_of[bt][:, :, jc * P : (jc + 1) * P], in1=e_of[c][:], op=ALU.mult
             )
             enc_e_of[c] = enc_e
 
-        def idle_pass(out):
-            nc.tensor.matmul_mx(
-                out=out,
-                lhsT=attn_w_q[0][:, 0, :].bitcast(FP8X4),
-                lhsT_scale=attn_w_q[1][:, 0, :],
-                rhs=x_q[0][:, 0, :].bitcast(FP8X4),
-                rhs_scale=x_q[1][:, 0, :],
-                start=True,
-                stop=True,
-            )
-
-        def sum_over_s(c, run):
-            if run == 0:
-                if c % JC_PER_BANK == 0:
-                    sums_ps = psum_sums.tile([P, 2, JC_PER_BANK, P], F32, tag="sums")
-                    bank_of[c // JC_PER_BANK] = sums_ps
-                place = c % JC_PER_BANK
-                pair = bank_of[c // JC_PER_BANK]
-                sums_of[c] = (pair[:, 0, place, :], pair[:, 1, place, :])
-            terms = [(i, tile, s) for i, tile in enumerate((e_of[c], enc_e_of[c])) for s in range(S)]
-            for i, tile, s in terms[run * RUN : (run + 1) * RUN]:
+        def sum_over_s(c, which):
+            if which == 0 and c % JC_PER_BANK == 0:
+                sums_ps = psum_sums.tile([P, 2, JC_PER_BANK, P], F32, tag="sums")
+                bank_of[c // JC_PER_BANK] = sums_ps
+            terms = (e_of, enc_e_of)[which][c]
+            for s in range(S):
                 nc.tensor.matmul(
-                    out=sums_of[c][i],
-                    lhsT=tile[:, s, :],
+                    out=bank_of[c // JC_PER_BANK][:, which, c % JC_PER_BANK, :],
+                    lhsT=terms[:, s, :],
                     rhs=ident_f32[:],
-                    is_transpose=True,
+                    is_transpose=s != S // 2,
                     start=(s == 0),
                     stop=(s == S - 1),
                 )
@@ -272,10 +253,11 @@ def tile_decoderlstm_pa_t_kernel(
 
         def bank(bt, k):
             if bt == N_BT - 1 and k > 0:
-                e_sum, enc_e_sum = sums_of[LAST - 1]
-                return slice(JC_PER_BANK, N_JC - 1), e_sum.unsqueeze(1), enc_e_sum.unsqueeze(1)
-            pair = bank_of[2 * bt + k]
-            return slice(k * JC_PER_BANK, (k + 1) * JC_PER_BANK), pair[:, 0, :, :], pair[:, 1, :, :]
+                n_chunks = JC_PER_BANK - 1
+            else:
+                n_chunks = JC_PER_BANK
+            sums = bank_of[2 * bt + k][:, :, 0:n_chunks, :]
+            return slice(k * JC_PER_BANK, k * JC_PER_BANK + n_chunks), sums[:, 0, :, :], sums[:, 1, :, :]
 
         def log_of_e_sum(bt):
             inv_t = row_pool.tile([P, N_JC, P], F32)
@@ -362,7 +344,7 @@ def tile_decoderlstm_pa_t_kernel(
                 gates_ps = psum_move.tile([P, N_GATES, P], F32, tag="move")
             gates_of[n] = gates_ps
 
-        def gate_product(n, gate):
+        def gate_products(n, gates):
             bt, jc = divmod(n, N_JC)
             att_words, att_scales = cell_of[bt, "att_q"]
             products = (
@@ -370,17 +352,18 @@ def tile_decoderlstm_pa_t_kernel(
                 (w_h_q, h_q[0][:, bt, :], h_q[1][:, bt, :]),
                 (w_att_q, att_words[:], att_scales[:]),
             )
-            gc = gate * N_JC + jc
-            for i, (weights, v_words, v_scales) in enumerate(products):
-                nc.tensor.matmul_mx(
-                    out=gates_of[n][:, gate, :],
-                    lhsT=weights[0][:, gc, :].bitcast(FP8X4),
-                    lhsT_scale=weights[1][:, gc, :],
-                    rhs=v_words.bitcast(FP8X4),
-                    rhs_scale=v_scales,
-                    start=(i == 0),
-                    stop=(i == len(products) - 1),
-                )
+            for gate in gates:
+                gc = gate * N_JC + jc
+                for i, (weights, v_words, v_scales) in enumerate(products):
+                    nc.tensor.matmul_mx(
+                        out=gates_of[n][:, gate, :],
+                        lhsT=weights[0][:, gc, :].bitcast(FP8X4),
+                        lhsT_scale=weights[1][:, gc, :],
+                        rhs=v_words.bitcast(FP8X4),
+                        rhs_scale=v_scales,
+                        start=(i == 0),
+                        stop=(i == len(products) - 1),
+                    )
 
         def tanh_of_gates(n):
             bt, jc = divmod(n, N_JC)
@@ -404,40 +387,28 @@ def tile_decoderlstm_pa_t_kernel(
 
         def cell_inputs(n):
             bt, jc = divmod(n, N_JC)
-            if n >= SBUF_JOBS:
-                return
-            nc.tensor.matmul(
-                out=tanh_g_ps(n),
-                lhsT=ident_f32[:],
-                rhs=cell_of[bt, "tanh"][GATE_G][:, jc, :],
-                start=True,
-                stop=True,
-            )
-
-        def transpose_c(n):
-            bt, jc = divmod(n, N_JC)
+            if n < SBUF_JOBS:
+                nc.tensor.matmul(
+                    out=tanh_g_ps(n),
+                    lhsT=ident_f32[:],
+                    rhs=cell_of[bt, "tanh"][GATE_G][:, jc, :],
+                    start=True,
+                    stop=True,
+                )
             nc.tensor.transpose(c_t_ps(n), cell_of[bt, "c_raw"][:, jc * P : (jc + 1) * P], ident_bf[:])
 
-        def transpose_states(jobs):
-            if not jobs:
-                return
-            if jobs[0] < SBUF_JOBS:
-                states_ps = psum_move.tile([P, 2, 2, P], F32, tag="move")
+        def transpose_state(n):
+            bt, jc = divmod(n, N_JC)
+            if n < SBUF_JOBS:
+                state_ps = psum_move.tile([P, 2, P], F32, tag="move")
             else:
-                states_ps = psum_sums.tile([P, 2, 2, P], F32, tag="sums")
-            for place, n in enumerate(jobs):
-                bt, jc = divmod(n, N_JC)
-                for i, term in enumerate(terms_of[n]):
-                    nc.tensor.matmul(
-                        out=states_ps[:, place, 0, :],
-                        lhsT=term[:],
-                        rhs=ident_f32[:],
-                        is_transpose=True,
-                        start=(i == 0),
-                        stop=(i == 1),
-                    )
-                nc.tensor.transpose(states_ps[:, place, 1, :], cell_of[bt, "tanh"][GATE_O][:, jc, :], ident_f32[:])
-                cell_of[n, "state_ps"] = states_ps[:, place, :, :]
+                state_ps = psum_sums.tile([P, 2, P], F32, tag="sums")
+            for i, term in enumerate(terms_of[n]):
+                nc.tensor.matmul(
+                    out=state_ps[:, 0, :], lhsT=term[:], rhs=ident_f32[:], is_transpose=True, start=(i == 0), stop=(i == 1)
+                )
+            nc.tensor.transpose(state_ps[:, 1, :], cell_of[bt, "tanh"][GATE_O][:, jc, :], ident_f32[:])
+            cell_of[n, "state_ps"] = state_ps
 
         def kept_and_fresh(n):
             bt, jc = divmod(n, N_JC)
@@ -509,12 +480,6 @@ def tile_decoderlstm_pa_t_kernel(
         raw_of = {}
 
         transposed_in = [-1, -1, 0, 0, 1, 1, 2, 2, 3, 3, 4, 4, 5, 5, 6]
-        jobs_of = {}
-        for n in range(N_CHUNKS):
-            jobs_of.setdefault(max(n + 9, transposed_in[-1] + 2 + n // 2), []).append(n)
-
-        def jobs_in(step):
-            return jobs_of.get(step, [])
 
         def for_chunk(c, *stages):
             if 0 <= c < N_CHUNKS:
@@ -526,22 +491,6 @@ def tile_decoderlstm_pa_t_kernel(
             if jc == 0 and 0 <= bt < N_BT:
                 for stage in stages:
                     stage(bt)
-
-        def keep_multiplying(step, block, columns, target):
-            if is_chunk(step - 2) and is_chunk(step):
-                while columns < (QUOTA if jobs_in(step) else EARLY_QUOTA)[block]:
-                    idle_pass(target)
-                    columns += PASS_COLUMNS
-
-        def multiply_and_sum(step, run, columns, gates_to_do):
-            jobs = jobs_in(step)
-            columns += 3 * PASS_COLUMNS * len(gates_to_do) * len(jobs)
-            if jobs or is_chunk(step - 2):
-                keep_multiplying(step, run, columns, gates_of[jobs[-1] if jobs else None][:, gates_to_do[-1], :])
-            for n in jobs:
-                for gate in gates_to_do:
-                    gate_product(n, gate)
-            for_chunk(step - 2, lambda c: sum_over_s(c, run))
 
         def is_chunk(c):
             return 0 <= c < N_CHUNKS
@@ -572,63 +521,50 @@ def tile_decoderlstm_pa_t_kernel(
             for group in first:
                 quantise(group)
 
-            def for_jobs(step, *stages):
-                for n in jobs_in(step):
-                    for stage in stages:
-                        stage(n)
-
             for step in range(-4, N_CHUNKS):
-                if not jobs_in(step) and is_chunk(step - 2):
-                    open_gates(None)
-                for n in jobs_in(step):
-                    open_gates(n)
-                    if n % N_JC == 0:
-                        load_c(n // N_JC)
+                job = step - FIRST_JOB_STEP
+                for_chunk(job, open_gates)
+                for_tile(job, load_c)
                 for_tile(step - 6, one_over_e_sum)
                 for_chunk(step, max_into_psum)
                 for_parts(step, transpose_part)
-                multiply_and_sum(step, 0, 4 * PASS_COLUMNS, (0, 1))
+                for_chunk(job, lambda n: gate_products(n, (0, 1)))
+                for_chunk(step - 2, lambda c: sum_over_s(c, 0))
                 for_tile(step - 7, attention_rows)
+                for_chunk(job, lambda n: gate_products(n, (2, 3)))
                 for_chunk(step + 1, scores)
-                for_jobs(step - 3, new_output)
+                for_chunk(job - 1, cell_inputs)
+                for_chunk(job - 3, new_output)
                 for_chunk(step, subtract_max)
-                for_jobs(step - 2, kept_and_fresh)
+                for_chunk(job - 2, kept_and_fresh)
                 for_chunk(step + 1, max_over_s)
                 for_tile(step - 8, quantise_attention)
                 for_parts(step, quantise_if_last)
                 for_chunk(step, exponential)
-                multiply_and_sum(step, 1, 0, (2, 3))
-                keep_multiplying(step, 2, 4 * PASS_COLUMNS * (1 + len(jobs_in(step - 1))), row_ps(step + 2))
+                for_chunk(job - 2, transpose_state, new_state)
                 for_chunk(step + 2, lin_into_psum)
-                for_jobs(step - 1, cell_inputs, transpose_c)
-                transpose_states(jobs_in(step - 2))
-                for_jobs(step - 2, new_state)
+                for_chunk(step - 2, lambda c: sum_over_s(c, 1))
                 for_tile(step - 7, group_attention)
                 for_tile(step - 6, attention)
                 for_chunk(step - 1, weigh_enc)
-                for_jobs(step, tanh_of_gates)
+                for_chunk(job, tanh_of_gates)
                 for_parts(step + 1, pair_part)
                 for_parts(step + 2, load_part)
                 for_tile(step - 5, log_of_e_sum)
                 for_tile(step + 4, load_enc, attn_lin)
 
             last_bt = N_BT - 1
-            first_job = N_CHUNKS - 9
+            first_job = N_CHUNKS - FIRST_JOB_STEP
 
-            def start_job(n, gates_to_do):
-                if is_chunk(n):
-                    if gates_to_do[0] == 0:
-                        if n % N_JC == 0:
-                            load_c(n // N_JC)
-                        open_gates(n)
-                    for gate in gates_to_do:
-                        gate_product(n, gate)
+            def start_job(n):
+                for_tile(n, load_c)
+                for_chunk(n, open_gates, lambda m: gate_products(m, range(N_GATES)))
 
             def finish_jobs(n):
                 if n > first_job:
-                    for_chunk(n - 3, lambda m: transpose_states([m]), new_state)
+                    for_chunk(n - 3, transpose_state, new_state)
                 for_chunk(n - 3 if n == first_job else n - 4, new_output)
-                for_chunk(n - 1, cell_inputs, transpose_c)
+                for_chunk(n - 1, cell_inputs)
                 for_chunk(n - 2, kept_and_fresh)
 
             last_sums.append(sum_by_vector(e_of[LAST]))
@@ -637,16 +573,16 @@ def tile_decoderlstm_pa_t_kernel(
             sum_over_s(LAST - 1, 0)
             log_of_e_sum(last_bt)
             one_over_e_sum(last_bt)
-            start_job(first_job, range(N_GATES))
+            start_job(first_job)
             sum_over_s(LAST - 1, 1)
             tanh_of_gates(first_job)
             finish_jobs(first_job)
             last_sums.append(sum_by_vector(enc_e_of[LAST]))
-            start_job(first_job + 1, range(N_GATES))
+            start_job(first_job + 1)
             tanh_of_gates(first_job + 1)
             attention(last_bt)
             last_attention_by_vector()
-            start_job(first_job + 2, range(N_GATES))
+            start_job(first_job + 2)
             attention_rows(last_bt)
             group_attention(last_bt)
             quantise_attention(last_bt)
@@ -654,6 +590,6 @@ def tile_decoderlstm_pa_t_kernel(
             tanh_of_gates(first_job + 2)
             finish_jobs(first_job + 2)
             for n in range(first_job + 3, N_CHUNKS + 4):
-                start_job(n, range(N_GATES))
+                start_job(n)
                 finish_jobs(n)
                 for_chunk(n, tanh_of_gates)

@@ -120,9 +120,9 @@ def tile_decoderlstm_pa_t_kernel(
             )
             return raw
 
-        def part_pairs(raw):
+        def part_pairs(raw, copy):
             pairs = pairs_pool.tile([P, PART, 2, P], F32)
-            nc.scalar.copy(out=pairs[:], in_=raw[:].bitcast(F32).rearrange("p a (w u) -> p a u w", u=2))
+            copy(out=pairs[:], in_=raw[:].bitcast(F32).rearrange("p a (w u) -> p a u w", u=2))
             return pairs
 
         def bring_k_to_partitions(group, part, raw, copy):
@@ -184,7 +184,14 @@ def tile_decoderlstm_pa_t_kernel(
 
         def lin_into_psum(c):
             bt, jc = divmod(c, N_JC)
-            nc.tensor.matmul(out=row_ps(c), lhsT=lin_t_of[bt][:, jc, :], rhs=ident_f32[:], start=True, stop=True)
+            nc.tensor.matmul(
+                out=row_ps(c),
+                lhsT=lin_t_of[bt][:, jc, :],
+                rhs=ident_f32[:],
+                is_transpose=c - 2 < FIRST_JOB_STEP,
+                start=True,
+                stop=True,
+            )
 
         def scores(c):
             bt, jc = divmod(c, N_JC)
@@ -244,7 +251,7 @@ def tile_decoderlstm_pa_t_kernel(
                     out=bank_of[c // JC_PER_BANK][:, which, c % JC_PER_BANK, :],
                     lhsT=terms[:, s, :],
                     rhs=ident_f32[:],
-                    is_transpose=s != S // 2,
+                    is_transpose=s != S // 2 or c + 2 < FIRST_JOB_STEP,
                     start=(s == 0),
                     stop=(s == S - 1),
                 )
@@ -507,7 +514,7 @@ def tile_decoderlstm_pa_t_kernel(
             bring_k_to_partitions(group, part, raw_of[group[0], part], nc.scalar.copy)
 
         def pair_part(group, part):
-            raw_of[group[0], part] = part_pairs(raw_of[group[0], part])
+            raw_of[group[0], part] = part_pairs(raw_of[group[0], part], nc.scalar.copy)
 
         def quantise_if_last(group, part):
             if part == group[-1] // PART - 1:
@@ -515,9 +522,10 @@ def tile_decoderlstm_pa_t_kernel(
 
         with tc.manual_schedule():
             first_raw = [load_rows(group, 0) for group in first]
-            first_raw = [part_pairs(raw) for raw in first_raw]
-            for group, raw, copy in zip(first, first_raw, (nc.scalar.copy, nc.vector.tensor_copy)):
-                bring_k_to_partitions(group, 0, raw, copy)
+            copies = (nc.scalar.copy, nc.vector.tensor_copy)
+            first_pairs = [part_pairs(raw, nc.vector.tensor_copy) for raw in first_raw]
+            for group, pairs, copy in zip(first, first_pairs, copies):
+                bring_k_to_partitions(group, 0, pairs, copy)
             for group in first:
                 quantise(group)
 
@@ -586,10 +594,23 @@ def tile_decoderlstm_pa_t_kernel(
             attention_rows(last_bt)
             group_attention(last_bt)
             quantise_attention(last_bt)
-            finish_jobs(first_job + 1)
-            tanh_of_gates(first_job + 2)
-            finish_jobs(first_job + 2)
-            for n in range(first_job + 3, N_CHUNKS + 4):
+            start_job(first_job + 3)
+            for n in range(first_job + 1, first_job + 4):
+                finish_jobs(n)
+                if n > first_job + 1:
+                    tanh_of_gates(n)
+            for n in range(first_job + 4, N_CHUNKS):
                 start_job(n)
                 finish_jobs(n)
-                for_chunk(n, tanh_of_gates)
+                tanh_of_gates(n)
+            cell_inputs(LAST)
+            kept_and_fresh(LAST - 1)
+            transpose_state(LAST - 2)
+            new_state(LAST - 2)
+            new_output(LAST - 3)
+            kept_and_fresh(LAST)
+            for n in range(LAST - 1, N_CHUNKS):
+                transpose_state(n)
+                new_state(n)
+                new_output(n - 1)
+            new_output(LAST)

@@ -212,19 +212,23 @@ def tile_decoderlstm_pa_t_kernel(
         def max_into_psum(c):
             nc.tensor.matmul(out=row_ps(c), lhsT=ident_f32[:], rhs=top_of[c][:], start=True, stop=True)
 
+        def n_for_vector(c):
+            return 7 if c < FIRST_JOB_STEP + 2 else (6, 5)[c % 2]
+
         def subtract_max(c):
-            for_vector = scores_of[c][:, 0:S_OUT_VECTOR, :, :]
+            n = n_for_vector(c)
+            for_vector = scores_of[c][:, 0:n, :, :]
             nc.vector.tensor_tensor(
-                out=for_vector, in0=for_vector, in1=for_s(row_ps(c), S_OUT_VECTOR), op=ALU.subtract
+                out=for_vector, in0=for_vector, in1=for_s(row_ps(c), n), op=ALU.subtract
             )
-            for_gpsimd = scores_of[c][:, S_OUT_VECTOR:S_OUT, :, :]
+            for_gpsimd = scores_of[c][:, n:S_OUT, :, :]
             nc.gpsimd.tensor_tensor(
-                out=for_gpsimd, in0=for_gpsimd, in1=for_s(top_of[c][:], S_OUT - S_OUT_VECTOR), op=ALU.subtract
+                out=for_gpsimd, in0=for_gpsimd, in1=for_s(top_of[c][:], S_OUT - n), op=ALU.subtract
             )
 
         def exponential(c):
             e = e_pool.tile([P, S, P], F32)
-            for o_range in (slice(S_OUT_VECTOR, S_OUT), slice(0, S_OUT_VECTOR)):
+            for o_range in (slice(n_for_vector(c), S_OUT), slice(0, n_for_vector(c))):
                 nc.scalar.activation(
                     out=e[:].rearrange("p (o r) j -> p o j r", r=S_RUN)[:, o_range, :, :],
                     in_=scores_of[c][:, o_range, :, :],

from contextlib import ExitStack

import concourse.mybir as mybir
from concourse.masks import make_identity

BF16 = mybir.dt.bfloat16
F32 = mybir.dt.float32
U32 = mybir.dt.uint32
U8 = mybir.dt.uint8
I32 = mybir.dt.int32
FP8X4 = mybir.dt.float8_e4m3fn_x4
ALU = mybir.AluOpType
FUNC = mybir.ActivationFunctionType
INNER_TWO = mybir.AxisListType.XY

P = 128
PACK = 4
PART = 4
K_PASS = P * PACK
PAIRS = K_PASS // 2
B, H, S = 1024, 512, 16
N_BT = B // P
N_JC = H // P
N_CHUNKS = N_BT * N_JC
LAST = N_CHUNKS - 1
SBUF_JOBS = N_CHUNKS - 8
FREE_BANK_JOB = N_CHUNKS - 7
FIRST_JOB_STEP = 9
N_GATES = 4
GATE_I, GATE_F, GATE_G, GATE_O = 0, 1, 2, 3
N_GC = N_GATES * N_JC
S_RUN = 2
S_OUT = S // S_RUN
S_OUT_VECTOR = 5
JC_PER_BANK = N_JC // 2
GATE_SCALE = (0.5, 0.5, 1.0, 0.5)

FLOPS = 2 * B * H * H + 2 * B * (3 * H) * (N_GATES * H)


def tile_decoderlstm_pa_t_kernel(
    tc, x, enc_seq, attn_W, attn_b, h_prev, c_prev, W_ih0, W_hh0, b_ih0, b_hh0, out_0, out_1
):
    nc = tc.nc
    with ExitStack() as ctx:
        keep = ctx.enter_context(tc.tile_pool(name="keep", bufs=1))
        raw_pool = ctx.enter_context(tc.tile_pool(name="raw", bufs=3))
        pairs_pool = ctx.enter_context(tc.tile_pool(name="pairs", bufs=3))
        grouped_pool = ctx.enter_context(tc.tile_pool(name="grouped", bufs=2))
        enc_pool = ctx.enter_context(tc.tile_pool(name="enc", bufs=2))
        scores_pool = ctx.enter_context(tc.tile_pool(name="scores", bufs=3))
        top_pool = ctx.enter_context(tc.tile_pool(name="top", bufs=3))
        e_pool = ctx.enter_context(tc.tile_pool(name="e", bufs=3))
        prod_pool = ctx.enter_context(tc.tile_pool(name="prod", bufs=3))
        row_pool = ctx.enter_context(tc.tile_pool(name="row", bufs=2))
        att_pool = ctx.enter_context(tc.tile_pool(name="att", bufs=4))
        cell_pool = ctx.enter_context(tc.tile_pool(name="cell", bufs=2))
        out_pool = ctx.enter_context(tc.tile_pool(name="out", bufs=2))
        psum_row = ctx.enter_context(tc.psum_pool(name="psum_row", bufs=1))
        psum_sums = ctx.enter_context(tc.psum_pool(name="psum_sums", bufs=3))
        psum_move = ctx.enter_context(tc.psum_pool(name="psum_move", bufs=3))

        ident_bf = keep.tile([P, P], BF16)
        make_identity(nc, ident_bf[:])
        ident_f32 = keep.tile([P, P], F32)
        make_identity(nc, ident_f32[:])
        rows_even_ps = psum_row.tile([P, 3, P], F32)
        rows_odd_ps = psum_row.tile([P, 3, P], F32)
        both_rows_ps = (rows_even_ps, rows_odd_ps)

        def row_ps(c):
            return both_rows_ps[c % 2][:, 0, :]

        def tanh_g_ps(n):
            return both_rows_ps[(n + 1) % 2][:, 1, :]

        def c_t_ps(n):
            return both_rows_ps[(n + 1) % 2][:, 2, :].bitcast(BF16)[:, 0:P]

        bias_rows = keep.tile([P, P], BF16)
        nc.vector.memset(bias_rows[:].bitcast(I32), 0)
        nc.sync.dma_start(out=bias_rows[0:N_GC, :], in_=b_ih0.rearrange("(r c) -> r c", c=P))
        nc.sync.dma_start(out=bias_rows[N_GC : 2 * N_GC, :], in_=b_hh0.rearrange("(r c) -> r c", c=P))
        nc.sync.dma_start(
            out=bias_rows[2 * N_GC : 2 * N_GC + N_JC, :], in_=attn_b.rearrange("(r c) -> r c", c=P)
        )
        bias_ps = psum_move.tile([P, P], BF16, tag="move")
        nc.tensor.transpose(bias_ps[:], bias_rows[:], ident_bf[:])
        bias_cols = keep.tile([P, P], F32)
        nc.scalar.copy(out=bias_cols[:], in_=bias_ps[:])
        attn_bias = bias_cols[:, 2 * N_GC : 2 * N_GC + N_JC]
        gate_bias = keep.tile([P, N_GC], F32)
        nc.vector.tensor_tensor(
            out=gate_bias[:], in0=bias_cols[:, 0:N_GC], in1=bias_cols[:, N_GC : 2 * N_GC], op=ALU.add
        )
        for gate in range(N_GATES):
            cols = slice(gate * N_JC, (gate + 1) * N_JC)
            nc.vector.tensor_scalar_mul(out=gate_bias[:, cols], in0=gate_bias[:, cols], scalar1=GATE_SCALE[gate])

        def operand_tiles(n_chunks, label):
            words = keep.tile([P, n_chunks, P], U32, name=label + "_words", align_bytes=64)
            scales = keep.tile([P, n_chunks, P], U8, name=label + "_scales", align_bytes=64)
            return words, scales

        x_q = operand_tiles(N_BT, "x")
        h_q = operand_tiles(N_BT, "h")
        attn_w_q = operand_tiles(N_JC, "attn_w")
        w_x_q = operand_tiles(N_GC, "w_x")
        w_att_q = operand_tiles(N_GC, "w_att")
        w_h_q = operand_tiles(N_GC, "w_h")

        grouped_of = {}

        def load_rows(group, part):
            name, matrix, k_cols, operand, first_chunk, n_chunks = group
            first_row = (first_chunk + part * PART) * P
            raw = raw_pool.tile([P, PART, K_PASS], BF16)
            nc.sync.dma_start(
                out=raw[:], in_=matrix[first_row : first_row + PART * P, k_cols].rearrange("(a r) k -> r a k", r=P)
            )
            return raw

        def part_pairs(raw, copy):
            pairs = pairs_pool.tile([P, PART, 2, P], F32)
            copy(out=pairs[:], in_=raw[:].bitcast(F32).rearrange("p a (w u) -> p a u w", u=2))
            return pairs

        def bring_k_to_partitions(group, part, raw, copy):
            if part == 0:
                grouped = grouped_pool.tile([P, group[-1], P, PACK], BF16, align_bytes=64)
                grouped_of[group[0]] = grouped
            grouped_pairs = grouped_of[group[0]][:, part * PART : (part + 1) * PART, :, :].bitcast(F32)
            for a0 in range(0, PART, 2):
                k_first = psum_move.tile([P, 2, 2, P], F32, tag="move")
                for a in range(2):
                    for u in range(2):
                        nc.tensor.transpose(k_first[:, a, u, :], raw[:, a0 + a, u, :], ident_f32[:])
                copy(out=grouped_pairs[:, a0 : a0 + 2, :, :], in_=k_first[:].rearrange("p a u r -> p a r u"))

        def quantise(group):
            name, matrix, k_cols, operand, first_chunk, n_chunks = group
            words, scales = operand
            chunks = slice(first_chunk, first_chunk + n_chunks)
            nc.vector.quantize_mx(
                out=words[:, chunks, :].rearrange("p a r -> p (a r)").bitcast(FP8X4),
                scales=scales[:, chunks, :].rearrange("p a r -> p (a r)"),
                in_=grouped_of[group[0]][:].rearrange("p a r t -> p (a r t)"),
            )

        enc_of, lin_t_of, scores_of, top_of, e_of, enc_e_of = {}, {}, {}, {}, {}, {}
        bank_of, gates_of, cell_of, terms_of = {}, {}, {}, {}

        def load_enc(bt):
            enc_sb = enc_pool.tile([P, S, H], BF16)
            nc.sync.dma_start(
                out=enc_sb[:], in_=enc_seq[:, bt * P : (bt + 1) * P, :].rearrange("s b j -> b s j")
            )
            enc_of[bt] = enc_sb

        def attn_lin(bt):
            lin_t_ps = psum_move.tile([P, N_JC, P], F32, tag="move")
            for jc in range(N_JC):
                nc.tensor.matmul_mx(
                    out=lin_t_ps[:, jc, :],
                    lhsT=attn_w_q[0][:, jc, :].bitcast(FP8X4),
                    lhsT_scale=attn_w_q[1][:, jc, :],
                    rhs=x_q[0][:, bt, :].bitcast(FP8X4),
                    rhs_scale=x_q[1][:, bt, :],
                    start=True,
                    stop=True,
                )
            lin_t = row_pool.tile([P, N_JC, P], F32)
            for jc in range(N_JC):
                nc.scalar.activation(
                    out=lin_t[:, jc, :], in_=lin_t_ps[:, jc, :], func=FUNC.Identity, bias=attn_bias[:, jc : jc + 1]
                )
            lin_t_of[bt] = lin_t

        def over_s(tile_ap):
            return tile_ap.rearrange("p o j r -> p j o r")

        def for_s(row_ap, n_out):
            return row_ap.unsqueeze(1).unsqueeze(3).to_broadcast([P, n_out, P, S_RUN])

        def lin_into_psum(c):
            bt, jc = divmod(c, N_JC)
            nc.tensor.matmul(
                out=row_ps(c),
                lhsT=lin_t_of[bt][:, jc, :],
                rhs=ident_f32[:],
                is_transpose=c - 2 < FIRST_JOB_STEP,
                start=True,
                stop=True,
            )

        def scores(c):
            bt, jc = divmod(c, N_JC)
            sc = scores_pool.tile([P, S_OUT, P, S_RUN], F32, tag="scores")
            nc.vector.tensor_tensor(
                out=sc[:],
                in0=for_s(row_ps(c), S_OUT),
                in1=enc_of[bt][:, :, jc * P : (jc + 1) * P].rearrange("p (o r) j -> p o j r", r=S_RUN),
                op=ALU.mult,
            )
            scores_of[c] = sc

        def max_over_s(c):
            top = top_pool.tile([P, P], F32)
            nc.vector.tensor_reduce(out=top[:], in_=over_s(scores_of[c][:]), axis=INNER_TWO, op=ALU.max)
            top_of[c] = top

        def max_into_psum(c):
            nc.tensor.matmul(out=row_ps(c), lhsT=ident_f32[:], rhs=top_of[c][:], start=True, stop=True)

        def n_for_vector(c):
            return 7 if c < FIRST_JOB_STEP + 2 else (6, 5)[c % 2]

        def subtract_max(c):
            n = n_for_vector(c)
            for_vector = scores_of[c][:, 0:n, :, :]
            nc.vector.tensor_tensor(
                out=for_vector, in0=for_vector, in1=for_s(row_ps(c), n), op=ALU.subtract
            )
            for_gpsimd = scores_of[c][:, n:S_OUT, :, :]
            nc.gpsimd.tensor_tensor(
                out=for_gpsimd, in0=for_gpsimd, in1=for_s(top_of[c][:], S_OUT - n), op=ALU.subtract
            )

        def exponential(c):
            e = e_pool.tile([P, S, P], F32)
            for o_range in (slice(n_for_vector(c), S_OUT), slice(0, n_for_vector(c))):
                nc.scalar.activation(
                    out=e[:].rearrange("p (o r) j -> p o j r", r=S_RUN)[:, o_range, :, :],
                    in_=scores_of[c][:, o_range, :, :],
                    func=FUNC.Exp,
                )
            e_of[c] = e

        def weigh_enc(c):
            bt, jc = divmod(c, N_JC)
            enc_e = prod_pool.tile([P, S, P], F32)
            engine = nc.vector if c >= LAST - 1 else nc.gpsimd
            engine.tensor_tensor(
                out=enc_e[:], in0=enc_of[bt][:, :, jc * P : (jc + 1) * P], in1=e_of[c][:], op=ALU.mult
            )
            enc_e_of[c] = enc_e

        def sum_over_s(c, which):
            if which == 0 and c % JC_PER_BANK == 0:
                sums_ps = psum_sums.tile([P, 2, JC_PER_BANK, P], F32, tag="sums")
                bank_of[c // JC_PER_BANK] = sums_ps
            terms = (e_of, enc_e_of)[which][c]
            for s in range(S):
                nc.tensor.matmul(
                    out=bank_of[c // JC_PER_BANK][:, which, c % JC_PER_BANK, :],
                    lhsT=terms[:, s, :],
                    rhs=ident_f32[:],
                    is_transpose=s != S // 2 or c + 2 < FIRST_JOB_STEP,
                    start=(s == 0),
                    stop=(s == S - 1),
                )

        last_sums = []

        def bank(bt, k):
            if bt == N_BT - 1 and k > 0:
                n_chunks = JC_PER_BANK - 1
            else:
                n_chunks = JC_PER_BANK
            sums = bank_of[2 * bt + k][:, :, 0:n_chunks, :]
            return slice(k * JC_PER_BANK, k * JC_PER_BANK + n_chunks), sums[:, 0, :, :], sums[:, 1, :, :]

        def log_of_e_sum(bt):
            inv_t = row_pool.tile([P, N_JC, P], F32)
            for k in range(2):
                jc, e_sum, enc_e_sum = bank(bt, k)
                nc.scalar.activation(out=inv_t[:, jc, :], in_=e_sum, func=FUNC.Ln)
            if bt == N_BT - 1:
                nc.scalar.activation(out=inv_t[:, N_JC - 1, :], in_=last_sums[0], func=FUNC.Ln)
            cell_of[bt, "inv_t"] = inv_t

        def one_over_e_sum(bt):
            inv_t = cell_of[bt, "inv_t"]
            nc.scalar.activation(out=inv_t[:], in_=inv_t[:], func=FUNC.Exp, scale=-1.0)

        def attention(bt):
            att_t = row_pool.tile([P, N_JC, P], BF16)
            for k in range(2):
                jc, e_sum, enc_e_sum = bank(bt, k)
                nc.vector.tensor_tensor(
                    out=att_t[:, jc, :], in0=enc_e_sum, in1=cell_of[bt, "inv_t"][:, jc, :], op=ALU.mult
                )
            cell_of[bt, "att_t"] = att_t

        def copy_for(bt):
            return nc.vector.tensor_copy if bt == N_BT - 1 else nc.scalar.copy

        def attention_rows(bt):
            n_jc = N_JC - 1 if bt == N_BT - 1 else N_JC
            att_ps = psum_move.tile([P, H], BF16, tag="move")
            for jc in range(n_jc):
                nc.tensor.transpose(att_ps[:, jc * P : (jc + 1) * P], cell_of[bt, "att_t"][:, jc, :], ident_bf[:])
            copy_for(bt)(out=att_tile(bt)[:, 0 : n_jc * P], in_=att_ps[:, 0 : n_jc * P])

        def att_tile(bt):
            if (bt, "att") not in cell_of:
                att = row_pool.tile([P, H], BF16)
                cell_of[bt, "att"] = att
            return cell_of[bt, "att"]

        def sum_by_vector(terms):
            sums = scores_pool.tile([P, S // 2, P], F32, tag="scores")
            n = S // 2
            while n > 0:
                nc.vector.tensor_tensor(out=sums[:, 0:n, :], in0=terms[:, 0:n, :], in1=terms[:, n : 2 * n, :], op=ALU.add)
                terms = sums
                n //= 2
            return sums[:, 0, :]

        def last_attention_by_vector():
            nc.vector.tensor_tensor(
                out=att_tile(N_BT - 1)[:, (N_JC - 1) * P : H],
                in0=last_sums[1],
                in1=cell_of[N_BT - 1, "inv_t"][:, N_JC - 1, :],
                op=ALU.mult,
            )

        def group_attention(bt):
            att_k_ps = psum_move.tile([P, PACK, P], BF16, tag="move")
            for t in range(PACK):
                nc.tensor.transpose(att_k_ps[:, t, :], cell_of[bt, "att"][:, t:H:PACK], ident_bf[:])
            att_grouped = row_pool.tile([P, P, PACK], BF16, align_bytes=64)
            copy_for(bt)(out=att_grouped[:], in_=att_k_ps[:].rearrange("p t b -> p b t"))
            cell_of[bt, "att_grouped"] = att_grouped

        def load_c(bt):
            c_raw = row_pool.tile([P, H], BF16)
            nc.sync.dma_start(out=c_raw[:], in_=c_prev[bt * P : (bt + 1) * P, :])
            cell_of[bt, "c_raw"] = c_raw

        def quantise_attention(bt):
            att_words = att_pool.tile([P, P], U32, align_bytes=64)
            att_scales = att_pool.tile([P, P], U8, align_bytes=64)
            nc.vector.quantize_mx(
                out=att_words[:].bitcast(FP8X4),
                scales=att_scales[:],
                in_=cell_of[bt, "att_grouped"][:].rearrange("p b t -> p (b t)"),
            )
            cell_of[bt, "att_q"] = (att_words, att_scales)

        def open_gates(n):
            if n == FREE_BANK_JOB:
                gates_ps = psum_sums.tile([P, N_GATES, P], F32, tag="sums")
            else:
                gates_ps = psum_move.tile([P, N_GATES, P], F32, tag="move")
            gates_of[n] = gates_ps

        def gate_products(n, gates):
            bt, jc = divmod(n, N_JC)
            att_words, att_scales = cell_of[bt, "att_q"]
            products = (
                (w_x_q, x_q[0][:, bt, :], x_q[1][:, bt, :]),
                (w_h_q, h_q[0][:, bt, :], h_q[1][:, bt, :]),
                (w_att_q, att_words[:], att_scales[:]),
            )
            for gate in gates:
                gc = gate * N_JC + jc
                for i, (weights, v_words, v_scales) in enumerate(products):
                    nc.tensor.matmul_mx(
                        out=gates_of[n][:, gate, :],
                        lhsT=weights[0][:, gc, :].bitcast(FP8X4),
                        lhsT_scale=weights[1][:, gc, :],
                        rhs=v_words.bitcast(FP8X4),
                        rhs_scale=v_scales,
                        start=(i == 0),
                        stop=(i == len(products) - 1),
                    )

        def tanh_of_gates(n):
            bt, jc = divmod(n, N_JC)
            if jc == 0:
                cell_of[bt, "tanh"] = [row_pool.tile([P, N_JC, P], F32, name="tanh_" + label) for label in "ifgo"]
            gates_ps = gates_of[n]
            for gate in range(N_GATES):
                gc = gate * N_JC + jc
                nc.scalar.activation(
                    out=cell_of[bt, "tanh"][gate][:, jc, :],
                    in_=gates_ps[:, gate, :],
                    func=FUNC.Tanh,
                    bias=gate_bias[:, gc : gc + 1],
                    scale=GATE_SCALE[gate],
                )
            tanh_o = cell_of[bt, "tanh"][GATE_O][:, jc, :]
            if bt == N_BT - 1:
                nc.vector.tensor_scalar_add(out=tanh_o, in0=tanh_o, scalar1=1.0)
            else:
                nc.scalar.add(out=tanh_o, in_=tanh_o, add=1.0)

        def cell_inputs(n):
            bt, jc = divmod(n, N_JC)
            if n < SBUF_JOBS:
                nc.tensor.matmul(
                    out=tanh_g_ps(n),
                    lhsT=ident_f32[:],
                    rhs=cell_of[bt, "tanh"][GATE_G][:, jc, :],
                    start=True,
                    stop=True,
                )
            nc.tensor.transpose(c_t_ps(n), cell_of[bt, "c_raw"][:, jc * P : (jc + 1) * P], ident_bf[:])

        def transpose_state(n):
            bt, jc = divmod(n, N_JC)
            if n < SBUF_JOBS:
                state_ps = psum_move.tile([P, 2, P], F32, tag="move")
            else:
                state_ps = psum_sums.tile([P, 2, P], F32, tag="sums")
            for i, term in enumerate(terms_of[n]):
                nc.tensor.matmul(
                    out=state_ps[:, 0, :], lhsT=term[:], rhs=ident_f32[:], is_transpose=True, start=(i == 0), stop=(i == 1)
                )
            nc.tensor.transpose(state_ps[:, 1, :], cell_of[bt, "tanh"][GATE_O][:, jc, :], ident_f32[:])
            cell_of[n, "state_ps"] = state_ps

        def kept_and_fresh(n):
            bt, jc = divmod(n, N_JC)
            tanh = cell_of[bt, "tanh"]
            kept = cell_pool.tile([P, P], F32)
            nc.vector.scalar_tensor_tensor(
                out=kept[:],
                in0=tanh[GATE_F][:, jc, :],
                scalar=1.0,
                in1=c_t_ps(n),
                op0=ALU.add,
                op1=ALU.mult,
            )
            fresh = cell_pool.tile([P, P], F32)
            nc.vector.scalar_tensor_tensor(
                out=fresh[:],
                in0=tanh[GATE_I][:, jc, :],
                scalar=1.0,
                in1=tanh[GATE_G][:, jc, :] if n >= SBUF_JOBS else tanh_g_ps(n),
                op0=ALU.add,
                op1=ALU.mult,
            )
            terms_of[n] = (kept, fresh)

        def new_state(n):
            bt, jc = divmod(n, N_JC)
            if jc == 0:
                c_new = out_pool.tile([P, H], F32)
                h_new = out_pool.tile([P, H], F32)
                cell_of[bt, "out"] = (c_new, h_new)
            c_new = cell_of[bt, "out"][0]
            c_twice_ps = cell_of[n, "state_ps"][:, 0, :]
            tanh_c = cell_pool.tile([P, P], F32)
            nc.scalar.activation(out=tanh_c[:], in_=c_twice_ps, func=FUNC.Tanh, scale=0.5)
            if bt == N_BT - 1:
                nc.vector.tensor_scalar_mul(out=c_new[:, jc * P : (jc + 1) * P], in0=c_twice_ps, scalar1=0.5)
            else:
                nc.scalar.mul(out=c_new[:, jc * P : (jc + 1) * P], in_=c_twice_ps, mul=0.5)
            cell_of[n, "tanh_c"] = tanh_c
            if jc == N_JC - 1:
                nc.sync.dma_start(out=out_1[bt * P : (bt + 1) * P, :], in_=c_new[:])

        def new_output(n):
            bt, jc = divmod(n, N_JC)
            h_new = cell_of[bt, "out"][1]
            nc.vector.scalar_tensor_tensor(
                out=h_new[:, jc * P : (jc + 1) * P],
                in0=cell_of[n, "state_ps"][:, 1, :],
                scalar=0.5,
                in1=cell_of[n, "tanh_c"][:],
                op0=ALU.mult,
                op1=ALU.mult,
            )
            if jc == N_JC - 1:
                nc.sync.dma_start(out=out_0[bt * P : (bt + 1) * P, :], in_=h_new[:])

        first_half = slice(0, H)
        second_half = slice(H, 2 * H)
        half_batch = N_BT // 2
        first = [("x0", x, first_half, x_q, 0, half_batch), ("attn_w", attn_W, first_half, attn_w_q, 0, N_JC)]
        later = [("x1", x, first_half, x_q, half_batch, half_batch), ("h", h_prev, first_half, h_q, 0, N_BT)]
        for half, first_chunk in (("0", 0), ("1", 8)):
            later += [
                ("w_x" + half, W_ih0, first_half, w_x_q, first_chunk, 8),
                ("w_h" + half, W_hh0, first_half, w_h_q, first_chunk, 8),
                ("w_att" + half, W_ih0, second_half, w_att_q, first_chunk, 8),
            ]
        parts = [(group, part) for group in later for part in range(group[-1] // PART)]
        raw_of = {}

        transposed_in = [-1, -1, 0, 0, 1, 1, 2, 2, 3, 3, 4, 4, 5, 5, 6]

        def for_chunk(c, *stages):
            if 0 <= c < N_CHUNKS:
                for stage in stages:
                    stage(c)

        def for_tile(first_chunk, *stages):
            bt, jc = divmod(first_chunk, N_JC)
            if jc == 0 and 0 <= bt < N_BT:
                for stage in stages:
                    stage(bt)

        def is_chunk(c):
            return 0 <= c < N_CHUNKS

        def for_parts(step, stage):
            for part, when in zip(parts, transposed_in):
                if when == step:
                    stage(*part)

        def load_part(group, part):
            raw_of[group[0], part] = load_rows(group, part)

        def transpose_part(group, part):
            bring_k_to_partitions(group, part, raw_of[group[0], part], nc.scalar.copy)

        def pair_part(group, part):
            raw_of[group[0], part] = part_pairs(raw_of[group[0], part], nc.scalar.copy)

        def quantise_if_last(group, part):
            if part == group[-1] // PART - 1:
                quantise(group)

        with tc.manual_schedule():
            first_raw = [load_rows(group, 0) for group in first]
            copies = (nc.scalar.copy, nc.vector.tensor_copy)
            first_pairs = [part_pairs(raw, nc.vector.tensor_copy) for raw in first_raw]
            for group, pairs, copy in zip(first, first_pairs, copies):
                bring_k_to_partitions(group, 0, pairs, copy)
            for group in first:
                quantise(group)

            for step in range(-4, N_CHUNKS):
                job = step - FIRST_JOB_STEP
                for_chunk(job, open_gates)
                for_tile(job, load_c)
                for_tile(step - 6, one_over_e_sum)
                for_chunk(step, max_into_psum)
                for_parts(step, transpose_part)
                for_chunk(job, lambda n: gate_products(n, (0, 1)))
                for_chunk(step - 2, lambda c: sum_over_s(c, 0))
                for_tile(step - 7, attention_rows)
                for_chunk(job, lambda n: gate_products(n, (2, 3)))
                for_chunk(step + 1, scores)
                for_chunk(job - 1, cell_inputs)
                for_chunk(job - 3, new_output)
                for_chunk(step, subtract_max)
                for_chunk(job - 2, kept_and_fresh)
                for_chunk(step + 1, max_over_s)
                for_tile(step - 8, quantise_attention)
                for_parts(step, quantise_if_last)
                for_chunk(step, exponential)
                for_chunk(job - 2, transpose_state, new_state)
                for_chunk(step + 2, lin_into_psum)
                for_chunk(step - 2, lambda c: sum_over_s(c, 1))
                for_tile(step - 7, group_attention)
                for_tile(step - 6, attention)
                for_chunk(step - 1, weigh_enc)
                for_chunk(job, tanh_of_gates)
                for_parts(step + 1, pair_part)
                for_parts(step + 2, load_part)
                for_tile(step - 5, log_of_e_sum)
                for_tile(step + 4, load_enc, attn_lin)

            last_bt = N_BT - 1
            first_job = N_CHUNKS - FIRST_JOB_STEP

            def start_job(n):
                for_tile(n, load_c)
                for_chunk(n, open_gates, lambda m: gate_products(m, range(N_GATES)))

            def finish_jobs(n):
                if n > first_job:
                    for_chunk(n - 3, transpose_state, new_state)
                for_chunk(n - 3 if n == first_job else n - 4, new_output)
                for_chunk(n - 1, cell_inputs)
                for_chunk(n - 2, kept_and_fresh)

            last_sums.append(sum_by_vector(e_of[LAST]))
            quantise_attention(last_bt - 1)
            weigh_enc(LAST)
            sum_over_s(LAST - 1, 0)
            log_of_e_sum(last_bt)
            one_over_e_sum(last_bt)
            start_job(first_job)
            sum_over_s(LAST - 1, 1)
            tanh_of_gates(first_job)
            finish_jobs(first_job)
            last_sums.append(sum_by_vector(enc_e_of[LAST]))
            start_job(first_job + 1)
            tanh_of_gates(first_job + 1)
            attention(last_bt)
            last_attention_by_vector()
            start_job(first_job + 2)
            attention_rows(last_bt)
            group_attention(last_bt)
            quantise_attention(last_bt)
            start_job(first_job + 3)
            for n in range(first_job + 1, first_job + 4):
                finish_jobs(n)
                if n > first_job + 1:
                    tanh_of_gates(n)
            for n in range(first_job + 4, N_CHUNKS):
                start_job(n)
                finish_jobs(n)
                tanh_of_gates(n)
            cell_inputs(LAST)
            kept_and_fresh(LAST - 1)
            transpose_state(LAST - 2)
            new_state(LAST - 2)
            new_output(LAST - 3)
            kept_and_fresh(LAST)
            for n in range(LAST - 1, N_CHUNKS):
                transpose_state(n)
                new_state(n)
                new_output(n - 1)
            new_output(LAST)
